import numpy as np
import ml_dtypes


def mxq(x, axis, fmt="e4m3"):
    dtype, down = {"e4m3": (ml_dtypes.float8_e4m3fn, 7), "e5m2": (ml_dtypes.float8_e5m2, 14)}[fmt]
    v = np.moveaxis(np.asarray(x, np.float32).astype(ml_dtypes.bfloat16).astype(np.float64), axis, -1)
    blocks = v.reshape(v.shape[:-1] + (-1, 32))
    amax = np.abs(blocks).max(-1, keepdims=True)
    byte = np.maximum(np.where(amax > 0, np.frexp(amax)[1] - 1 + 127, 0) - down, 1)
    scale = np.exp2(byte - 127.0)
    codes = (blocks / scale).astype(np.float32).astype(dtype).astype(np.float64)
    return np.moveaxis((codes * scale).reshape(v.shape), -1, axis)


WIDE = False


def mx_kscale(k):
    if not WIDE:
        return np.ones(k)
    levels = np.array([10, -10, 5, -5, 0])
    if k % 512:
        return np.exp2(np.random.permutation(np.resize(levels, k // 32))).repeat(32)
    a = np.empty((k // 512, 16))
    for p in range(k // 512):
        a[p, :8] = np.random.permutation(np.resize(levels, 8))
        for g in range(8):
            far = levels[np.abs(levels - a[p, g]) >= 10]
            a[p, g + 8] = far[np.random.randint(len(far))]
    return np.exp2(a.ravel()).repeat(32)


BF16 = ml_dtypes.bfloat16


def bf(x):
    return np.asarray(x, np.float32).astype(BF16)


def f64(x):
    return np.asarray(x).astype(np.float64)


B, D, H = 8192, 512, 8
DH = D // H
LN_EPS = 1e-5


def layernorm(x, g, b):
    mu = x.mean(-1, keepdims=True)
    var = ((x - mu) ** 2).mean(-1, keepdims=True)
    return (x - mu) / np.sqrt(var + LN_EPS) * g + b


def setup_inputs():
    s, t = mx_kscale(D), mx_kscale(D)
    return {"kv_in": bf(np.random.standard_normal((B, D)) * s),
            "q_in": bf(np.random.standard_normal((B, D))),
            "attn_w": bf(np.random.uniform(0.25, 1.0, (B, H, 1))),
            "w_v": bf(np.random.standard_normal((D, D)) / np.sqrt(D) / s[None, :] * t[:, None]),
            "b_v": bf(np.random.standard_normal(D) * 0.3 * t),
            "out_w": bf(np.random.standard_normal((D, D)) / np.sqrt(D) / t[None, :]),
            "out_b": bf(np.random.standard_normal(D) * 0.3),
            "ln_g": bf(1.0 + 0.1 * np.random.standard_normal(D)),
            "ln_b": bf(0.1 * np.random.standard_normal(D))}


def reference(kv_in, q_in, attn_w, w_v, b_v, out_w, out_b, ln_g, ln_b):
    v = ((mxq(f64(kv_in), 1, "e4m3") @ mxq(f64(w_v), 1, "e4m3").T) + f64(b_v)).reshape(B, H, DH)
    attn = (f64(attn_w) * v).reshape(B, D)
    y = (mxq(attn, 1, "e4m3") @ mxq(f64(out_w), 1, "e4m3").T) + f64(out_b)
    return layernorm(y + f64(q_in), f64(ln_g), f64(ln_b))

@@ -1,0 +1,385 @@
+from contextlib import ExitStack
+
+import concourse.mybir as mybir
+from concourse.masks import make_identity
+
+F32 = mybir.dt.float32
+BF16 = mybir.dt.bfloat16
+U32 = mybir.dt.uint32
+U8 = mybir.dt.uint8
+FP8X4 = mybir.dt.float8_e4m3fn_x4
+ALU = mybir.AluOpType
+ACT = mybir.ActivationFunctionType
+
+P = 128
+B = 8192
+D = 512
+NT = B // P
+GT = 2
+NG = NT // GT
+GW = GT * D
+GC = GT * P
+BLK = 8
+LN_EPS = 1e-5
+FLOPS = 2 * 2 * B * D * D
+PINNED = True
+G_COLS = 640
+
+
+def tile_crossmodalattention_pa_t_kernel(
+    tc, kv_in, q_in, attn_w, w_v, b_v, out_w, out_b, ln_g, ln_b, out
+):
+    nc = tc.nc
+    with ExitStack() as ctx:
+        if PINNED:
+            ctx.enter_context(tc.manual_schedule())
+        const = ctx.enter_context(tc.tile_pool(name="const", bufs=1))
+        w2 = ctx.enter_context(tc.tile_pool(name="w2", bufs=2))
+        w3 = ctx.enter_context(tc.tile_pool(name="w3", bufs=3))
+        w4 = ctx.enter_context(tc.tile_pool(name="w4", bufs=4))
+        psum = ctx.enter_context(tc.psum_pool(name="psum", bufs=1))
+
+        kv_view = kv_in.rearrange("(p j) k -> p (j k)", j=NT)
+        q_view = q_in.rearrange("(p j) k -> p (j k)", j=NT)
+        out_view = out.rearrange("(p j) n -> p (j n)", j=NT)
+
+        chunks = [(0, 2), (2, 8)] + [(a, a + 8) for a in range(8, NT, 8)]
+        kv_tiles = {}
+        q_tiles = {}
+
+        def load_chunk(view, store, prefix, k):
+            j0, j1 = chunks[k]
+            t = const.tile([P, (j1 - j0) * D], BF16, name="%s%d" % (prefix, k))
+            nc.sync.dma_start(out=t[:], in_=view[:, j0 * D : j1 * D])
+            for j in range(j0, j1):
+                store[j] = (t, (j - j0) * D)
+
+        eps = const.tile([P, 1], F32, name="eps")
+        nc.vector.memset(eps[:], LN_EPS)
+        warm = const.tile([P, 1], F32, name="warm")
+        nc.scalar.activation(out=warm[:], in_=eps[:], func=ACT.Abs_reciprocal_sqrt)
+        rows = const.tile([P, 3 * D], BF16, name="rows")
+        nc.vector.memset(rows[:], 0.0)
+        ones = const.tile([P, P], BF16, name="ones")
+        nc.vector.memset(ones[:], 1.0)
+        ident_f = const.tile([P, P], F32, name="ident_f")
+        make_identity(nc, ident_f[:])
+        ident_b = const.tile([P, P], BF16, name="ident_b")
+        make_identity(nc, ident_b[:])
+
+        load_chunk(kv_view, kv_tiles, "kv", 0)
+        aw_sb = const.tile([P, NT * 8], BF16, name="aw_sb")
+        nc.sync.dma_start(out=aw_sb[:], in_=attn_w.rearrange("(p j) h o -> p (j h o)", j=NT))
+        w_sb = const.tile([P, 4 * D], BF16, name="w_sb")
+        nc.sync.dma_start(out=w_sb[:], in_=w_v.rearrange("(p t) k -> p (t k)", t=4))
+        bv_bf = const.tile([P, 4], BF16, name="bv_bf")
+        nc.sync.dma_start(out=bv_bf[:], in_=b_v.rearrange("(p t) -> p t", t=4))
+        for i, vec in enumerate((ln_g, ln_b, out_b)):
+            nc.sync.dma_start(
+                out=rows[0:1, i * D : (i + 1) * D], in_=vec.rearrange("(o n) -> o n", o=1)
+            )
+        ow_sb = const.tile([P, 4 * D], BF16, name="ow_sb")
+        nc.sync.dma_start(
+            out=ow_sb[:].rearrange("p (nb d) -> p nb d", nb=4),
+            in_=out_w.rearrange("(nb p) d -> p nb d", p=P),
+        )
+        load_chunk(q_view, q_tiles, "q", 0)
+        load_chunk(kv_view, kv_tiles, "kv", 1)
+        load_chunk(q_view, q_tiles, "q", 1)
+        load_chunk(kv_view, kv_tiles, "kv", 2)
+        load_chunk(q_view, q_tiles, "q", 2)
+
+        def weight_words(words, tags, prefix):
+            grouped = const.tile([P, 4 * D], BF16, name=prefix + "g", align_bytes=64)
+            grouped_f = grouped[:].bitcast(F32)
+            for b in range(2):
+                bank = psum.tile([P, D], F32, name=prefix + "T%d" % b, tag=tags[b])
+                for s in range(2):
+                    for h in range(2):
+                        nc.tensor.transpose(
+                            bank[:, (s * 2 + h) * P : (s * 2 + h + 1) * P],
+                            words(2 * b + s, h),
+                            ident_f[:],
+                        )
+                nc.scalar.copy(
+                    out=grouped_f[:, b * D : (b + 1) * D].rearrange(
+                        "w (s c h) -> w s c h", s=2, h=2
+                    ),
+                    in_=bank[:].rearrange("w (s h c) -> w s c h", s=2, h=2),
+                )
+            return grouped
+
+        def quantise_weight(grouped, prefix):
+            codes = const.tile([P, D], U32, name=prefix + "c", align_bytes=64)
+            scales = const.tile([P, D], U8, name=prefix + "s", align_bytes=64)
+            nc.vector.quantize_mx(out=codes[:].bitcast(FP8X4), scales=scales[:], in_=grouped[:])
+            return codes, scales
+
+        def spread(i, tag, name):
+            bank = psum.tile([P, D], F32, name=name, tag=tag)
+            nc.tensor.matmul(
+                out=bank[:], lhsT=ones[:], rhs=rows[:, i * D : (i + 1) * D], start=True, stop=True
+            )
+            return bank
+
+        st = {}
+
+        def expand_head_weights(blk):
+            awx = w2.tile([P, BLK * P], BF16, name="awx", tag="awx")
+            nc.scalar.copy(
+                out=awx[:].rearrange("p (m r) -> p m r", r=16),
+                in_=aw_sb[:, blk * 64 : (blk + 1) * 64].unsqueeze(2).to_broadcast([P, 64, 16]),
+            )
+            st["awx", blk] = awx
+
+        def head_weights(blk):
+            awx = st["awx", blk]
+            awT = psum.tile([P, BLK * P], BF16, name="awT", tag="awT")
+            for j in range(BLK):
+                nc.tensor.transpose(
+                    awT[:, j * P : (j + 1) * P], awx[:, j * P : (j + 1) * P], ident_b[:]
+                )
+            awE = w2.tile([P, BLK * P], BF16, name="awE", tag="awE")
+            nc.scalar.copy(out=awE[:], in_=awT[:])
+            st["awE", blk] = awE
+
+        def residual(c):
+            qp = w3.tile([P, GW], F32, name="qp", tag="qp")
+            t, off = q_tiles[GT * c]
+            nc.vector.memset(qp[:, 0:1], 0.0)
+            nc.gpsimd.tensor_tensor(
+                out=qp[:].rearrange("p (j n) -> p j n", j=GT),
+                in0=t[:, off : off + GW].rearrange("p (j n) -> p j n", j=GT),
+                in1=ob_sb[:].unsqueeze(1).to_broadcast([P, GT, D]),
+                op=ALU.add,
+            )
+            st["qp", c] = qp
+
+        def to_quantise(tick):
+            if ("qin", tick) not in st:
+                st["qin", tick] = w3.tile([P, 8 * GC], BF16, name="qin", tag="qin", align_bytes=64)
+            return st["qin", tick]
+
+        def quantise(tick):
+            lo = 0 if tick < NG else GC
+            hi = 2 * GC if tick >= 2 else GC
+            codes = w2.tile([P, 2 * GC], U32, name="codes", tag="codes", align_bytes=64)
+            scales = w2.tile([P, 2 * GC], U8, name="scales", tag="scales", align_bytes=64)
+            nc.vector.quantize_mx(
+                out=codes[:, lo:hi].bitcast(FP8X4),
+                scales=scales[:, lo:hi],
+                in_=to_quantise(tick)[:, 4 * lo : 4 * hi],
+            )
+            st["codes", tick] = (codes, scales)
+
+        def transpose_kv(c):
+            kvT = psum.tile([P, D], F32, name="kvT", tag="kvT")
+            for jj in range(GT):
+                t, off = kv_tiles[GT * c + jj]
+                t_f = t[:].bitcast(F32)
+                for u in range(2):
+                    lo = off // 2
+                    nc.tensor.transpose(
+                        kvT[:, (jj * 2 + u) * P : (jj * 2 + u + 1) * P],
+                        t_f[:, lo + u : lo + 2 * P : 2],
+                        ident_f[:],
+                    )
+            nc.scalar.copy(
+                out=to_quantise(c)[:, 0 : 4 * GC]
+                .bitcast(F32)
+                .rearrange("w (s c h) -> w s c h", s=GT, h=2),
+                in_=kvT[:].rearrange("w (s h c) -> w s c h", s=GT, h=2),
+            )
+
+        def first_matmul(c):
+            codes, scales = st["codes", c]
+            banks = (
+                psum.tile([P, D], F32, name="s1a", tag="s1a"),
+                psum.tile([P, D], F32, name="s1b", tag="s1b"),
+            )
+            for t in range(4):
+                nc.tensor.matmul_mx(
+                    out=banks[t // 2][:, (t % 2) * GC : (t % 2 + 1) * GC],
+                    lhsT=wc[:, t * P : (t + 1) * P].bitcast(FP8X4),
+                    lhsT_scale=ws[:, t * P : (t + 1) * P],
+                    rhs=codes[:, 0:GC].bitcast(FP8X4),
+                    rhs_scale=scales[:, 0:GC],
+                    start=True,
+                    stop=True,
+                )
+            st["s1", c] = banks
+
+        def weigh_heads(c):
+            banks = st["s1", c]
+            awE = st["awE", (GT * c) // BLK]
+            lo = ((GT * c) % BLK) * P
+            planes = w2.tile([P, 4 * GC], BF16, name="planes", tag="planes")
+            for t in range(4):
+                nc.vector.scalar_tensor_tensor(
+                    out=planes[:, t * GC : (t + 1) * GC],
+                    in0=banks[t // 2][:, (t % 2) * GC : (t % 2 + 1) * GC],
+                    scalar=bv[:, t : t + 1],
+                    in1=awE[:, lo : lo + GC],
+                    op0=ALU.add,
+                    op1=ALU.mult,
+                )
+            nc.scalar.copy(
+                out=to_quantise(c + 2)[:, 4 * GC : 8 * GC].rearrange(
+                    "p (c i t) -> p c t i", i=4, t=4
+                ),
+                in_=planes[:].rearrange("p (t c i) -> p c t i", t=4, i=4),
+            )
+
+        def second_matmul(c):
+            codes, scales = st["codes", c + 2]
+            banks = (
+                psum.tile([P, D], F32, name="s2a", tag="s2a"),
+                psum.tile([P, D], F32, name="s2b", tag="s2b"),
+            )
+            for jj in range(GT):
+                nc.tensor.matmul_mx(
+                    out=banks[jj][:],
+                    lhsT=codes[:, GC + jj * P : GC + (jj + 1) * P].bitcast(FP8X4),
+                    lhsT_scale=scales[:, GC + jj * P : GC + (jj + 1) * P],
+                    rhs=oc[:].bitcast(FP8X4),
+                    rhs_scale=os_[:],
+                    start=True,
+                    stop=True,
+                )
+            st["s2", c] = banks
+
+        def add_residual(c):
+            banks = st["s2", c]
+            qp = st["qp", c]
+            z = w2.tile([P, GW], F32, name="z", tag="z")
+            sums = w2.tile([P, GT], F32, name="sums", tag="sums")
+            for jj in range(GT):
+                nc.vector.scalar_tensor_tensor(
+                    out=z[:, jj * D : (jj + 1) * D],
+                    in0=banks[jj][:],
+                    scalar=0.0,
+                    in1=qp[:, jj * D : (jj + 1) * D],
+                    op0=ALU.add,
+                    op1=ALU.add,
+                    accum_out=sums[:, jj : jj + 1],
+                )
+            negmu = w2.tile([P, GT], F32, name="negmu", tag="negmu")
+            nc.scalar.mul(out=negmu[:], in_=sums[:], mul=-1.0 / D)
+            ssq = w2.tile([P, GT], F32, name="ssq", tag="ssq")
+            for jj in range(GT):
+                junk = w2.tile([P, D], BF16, name="junk", tag="junk")
+                nc.scalar.activation(
+                    out=junk[:],
+                    in_=z[:, jj * D : (jj + 1) * D],
+                    func=ACT.Square,
+                    bias=negmu[:, jj : jj + 1],
+                    scale=1.0,
+                    accum_out=ssq[:, jj : jj + 1],
+                )
+            rstd = w2.tile([P, GT], F32, name="rstd", tag="rstd")
+            nc.scalar.activation(
+                out=rstd[:],
+                in_=ssq[:],
+                func=ACT.Abs_reciprocal_sqrt,
+                bias=eps[:, 0:1],
+                scale=1.0 / D,
+            )
+            st["z", c] = (z, negmu, rstd)
+
+        def gpsimd_cols(c):
+            lo = GW if c == NG - 1 else GW - G_COLS
+            return lo, GW
+
+        def centre(c):
+            z, negmu, rstd = st["z", c]
+            o = w4.tile([P, GW], F32, name="o", tag="o")
+            for jj in range(GT):
+                nc.vector.scalar_tensor_tensor(
+                    out=o[:, jj * D : (jj + 1) * D],
+                    in0=z[:, jj * D : (jj + 1) * D],
+                    scalar=negmu[:, jj : jj + 1],
+                    in1=g_ps[:],
+                    op0=ALU.add,
+                    op1=ALU.mult,
+                )
+            lo, hi = gpsimd_cols(c)
+            for jj in range(GT):
+                a, b = max(jj * D, lo), (jj + 1) * D
+                if a < b:
+                    nc.scalar.activation(
+                        out=o[:, a:b], in_=o[:, a:b], func=ACT.Copy, scale=rstd[:, jj : jj + 1]
+                    )
+            st["o", c] = o
+
+        def finish(c):
+            z, negmu, rstd = st["z", c]
+            o = st["o", c]
+            lo, hi = gpsimd_cols(c)
+            if lo < hi:
+                nc.gpsimd.tensor_tensor(
+                    out=o[:, lo:hi], in0=o[:, lo:hi], in1=b_sb[:, lo:hi], op=ALU.add
+                )
+            for jj in range(GT):
+                a, b = jj * D, min((jj + 1) * D, lo)
+                if a < b:
+                    nc.vector.scalar_tensor_tensor(
+                        out=o[:, a:b],
+                        in0=o[:, a:b],
+                        scalar=rstd[:, jj : jj + 1],
+                        in1=b_ps[:, 0 : b - a],
+                        op0=ALU.mult,
+                        op1=ALU.add,
+                    )
+            nc.sync.dma_start(out=out_view[:, c * GW : (c + 1) * GW], in_=o[:])
+
+        expand_head_weights(0)
+        transpose_kv(0)
+        w_f = w_sb[:].bitcast(F32)
+        wg = weight_words(
+            lambda t, u: w_f[:, t * 256 + u : (t + 1) * 256 : 2], ("s1a", "s1b"), "w"
+        )
+        wc, ws = quantise_weight(wg, "w")
+        head_weights(0)
+        bv = const.tile([P, 4], F32, name="bv")
+        nc.vector.tensor_copy(out=bv[:], in_=bv_bf[:])
+        ob_ps = spread(2, "kvT", "ob_ps")
+        ob_sb = const.tile([P, D], BF16, name="ob_sb")
+        nc.scalar.copy(out=ob_sb[:], in_=ob_ps[:])
+        g_ps = spread(0, "g_ps", "g_ps")
+        b_ps = spread(1, "b_ps", "b_ps")
+        ow_f = ow_sb[:].bitcast(F32).rearrange("n (nb q a) -> n nb a q", nb=4, a=2)
+        b_sb = const.tile([P, GW], F32, name="b_sb")
+
+        for tick in range(NG + 5):
+            if tick % 4 == 0 and tick // 4 + 3 < len(chunks):
+                load_chunk(kv_view, kv_tiles, "kv", tick // 4 + 3)
+                load_chunk(q_view, q_tiles, "q", tick // 4 + 3)
+            if tick + 1 < NG:
+                transpose_kv(tick + 1)
+            if (tick + 2) % 4 == 0 and (tick + 2) // 4 < NT // BLK:
+                head_weights((tick + 2) // 4)
+            if (tick + 3) % 4 == 0 and (tick + 3) // 4 < NT // BLK:
+                expand_head_weights((tick + 3) // 4)
+            if tick < NG:
+                residual(tick)
+            if tick < NG + 2:
+                quantise(tick)
+            if tick < NG:
+                first_matmul(tick)
+            if tick == 1:
+                oc, os_ = quantise_weight(og, "o")
+            if 0 <= tick - 2 < NG:
+                second_matmul(tick - 2)
+            if 0 <= tick - 4 < NG:
+                finish(tick - 4)
+            if 0 <= tick - 3 < NG:
+                centre(tick - 3)
+            if tick < NG:
+                weigh_heads(tick)
+            if 0 <= tick - 2 < NG:
+                add_residual(tick - 2)
+            if tick == 0:
+                og = weight_words(lambda nb, a: ow_f[:, nb, a, :], ("s2a", "s2b"), "o")
+                b2_ps = spread(1, "awT", "b2_ps")
+                for jj in range(GT):
+                    nc.scalar.copy(out=b_sb[:, jj * D : (jj + 1) * D], in_=b2_ps[:])

@@ -23,7 +23,6 @@ BLK = 8
 LN_EPS = 1e-5
 FLOPS = 2 * 2 * B * D * D
 PINNED = True
-G_COLS = 640
 
 
 def tile_crossmodalattention_pa_t_kernel(
@@ -143,17 +142,32 @@ def tile_crossmodalattention_pa_t_kernel(
             nc.scalar.copy(out=awE[:], in_=awT[:])
             st["awE", blk] = awE
 
-        def residual(c):
-            qp = w3.tile([P, GW], F32, name="qp", tag="qp")
+        def residual_tensor(c):
             t, off = q_tiles[GT * c]
-            nc.vector.memset(qp[:, 0:1], 0.0)
-            nc.gpsimd.tensor_tensor(
-                out=qp[:].rearrange("p (j n) -> p j n", j=GT),
-                in0=t[:, off : off + GW].rearrange("p (j n) -> p j n", j=GT),
-                in1=ob_sb[:].unsqueeze(1).to_broadcast([P, GT, D]),
-                op=ALU.add,
+            bank = psum.tile([P, D], F32, name="qb", tag="awT")
+            nc.tensor.matmul(
+                out=bank[:], lhsT=ident_b[:], rhs=t[:, off : off + D], start=True, stop=False
             )
-            st["qp", c] = qp
+            for n in range(4):
+                nc.tensor.matmul(
+                    out=bank[:, n * P : (n + 1) * P],
+                    lhsT=ob_cols[:, n * P : (n + 1) * P],
+                    rhs=ident_f[:],
+                    is_transpose=True,
+                    start=False,
+                    stop=n == 3,
+                )
+            qp0 = w3.tile([P, D], F32, name="qp0", tag="qp0")
+            nc.scalar.copy(out=qp0[:], in_=bank[:])
+            st["qp", c, 0] = qp0
+
+        def residual_gpsimd(c):
+            qp1 = w3.tile([P, D], F32, name="qp1", tag="qp1")
+            t, off = q_tiles[GT * c + 1]
+            nc.gpsimd.tensor_tensor(
+                out=qp1[:], in0=t[:, off : off + D], in1=ob_sb[:], op=ALU.add
+            )
+            st["qp", c, 1] = qp1
 
         def to_quantise(tick):
             if ("qin", tick) not in st:
@@ -209,25 +223,29 @@ def tile_crossmodalattention_pa_t_kernel(
                 )
             st["s1", c] = banks
 
-        def weigh_heads(c):
+        def add_value_bias(c):
             banks = st["s1", c]
+            planes = w2.tile([P, 4 * GC], F32, name="planes", tag="planes")
+            for t in range(4):
+                nc.scalar.activation(
+                    out=planes[:, t * GC : (t + 1) * GC],
+                    in_=banks[t // 2][:, (t % 2) * GC : (t % 2 + 1) * GC],
+                    func=ACT.Identity,
+                    bias=bv[:, t : t + 1],
+                    scale=1.0,
+                )
+            st["planes", c] = planes
+
+        def weigh_heads(c):
             awE = st["awE", (GT * c) // BLK]
             lo = ((GT * c) % BLK) * P
-            planes = w2.tile([P, 4 * GC], BF16, name="planes", tag="planes")
-            for t in range(4):
-                nc.vector.scalar_tensor_tensor(
-                    out=planes[:, t * GC : (t + 1) * GC],
-                    in0=banks[t // 2][:, (t % 2) * GC : (t % 2 + 1) * GC],
-                    scalar=bv[:, t : t + 1],
-                    in1=awE[:, lo : lo + GC],
-                    op0=ALU.add,
-                    op1=ALU.mult,
-                )
-            nc.scalar.copy(
-                out=to_quantise(c + 2)[:, 4 * GC : 8 * GC].rearrange(
-                    "p (c i t) -> p c t i", i=4, t=4
-                ),
-                in_=planes[:].rearrange("p (t c i) -> p c t i", t=4, i=4),
+            attn = to_quantise(c + 2)[:, 4 * GC : 8 * GC]
+            nc.vector.memset(attn[:, 0:2], 0.0)
+            nc.gpsimd.tensor_tensor(
+                out=attn.rearrange("p (n t) -> p n t", t=4),
+                in0=st["planes", c][:].rearrange("p (t n) -> p n t", t=4),
+                in1=awE[:, lo : lo + GC].unsqueeze(2).to_broadcast([P, GC, 4]),
+                op=ALU.mult,
             )
 
         def second_matmul(c):
@@ -250,7 +268,6 @@ def tile_crossmodalattention_pa_t_kernel(
 
         def add_residual(c):
             banks = st["s2", c]
-            qp = st["qp", c]
             z = w2.tile([P, GW], F32, name="z", tag="z")
             sums = w2.tile([P, GT], F32, name="sums", tag="sums")
             for jj in range(GT):
@@ -258,7 +275,7 @@ def tile_crossmodalattention_pa_t_kernel(
                     out=z[:, jj * D : (jj + 1) * D],
                     in0=banks[jj][:],
                     scalar=0.0,
-                    in1=qp[:, jj * D : (jj + 1) * D],
+                    in1=st["qp", c, jj][:],
                     op0=ALU.add,
                     op1=ALU.add,
                     accum_out=sums[:, jj : jj + 1],
@@ -286,10 +303,6 @@ def tile_crossmodalattention_pa_t_kernel(
             )
             st["z", c] = (z, negmu, rstd)
 
-        def gpsimd_cols(c):
-            lo = GW if c == NG - 1 else GW - G_COLS
-            return lo, GW
-
         def centre(c):
             z, negmu, rstd = st["z", c]
             o = w4.tile([P, GW], F32, name="o", tag="o")
@@ -302,34 +315,20 @@ def tile_crossmodalattention_pa_t_kernel(
                     op0=ALU.add,
                     op1=ALU.mult,
                 )
-            lo, hi = gpsimd_cols(c)
-            for jj in range(GT):
-                a, b = max(jj * D, lo), (jj + 1) * D
-                if a < b:
-                    nc.scalar.activation(
-                        out=o[:, a:b], in_=o[:, a:b], func=ACT.Copy, scale=rstd[:, jj : jj + 1]
-                    )
             st["o", c] = o
 
         def finish(c):
             z, negmu, rstd = st["z", c]
             o = st["o", c]
-            lo, hi = gpsimd_cols(c)
-            if lo < hi:
-                nc.gpsimd.tensor_tensor(
-                    out=o[:, lo:hi], in0=o[:, lo:hi], in1=b_sb[:, lo:hi], op=ALU.add
-                )
             for jj in range(GT):
-                a, b = jj * D, min((jj + 1) * D, lo)
-                if a < b:
-                    nc.vector.scalar_tensor_tensor(
-                        out=o[:, a:b],
-                        in0=o[:, a:b],
-                        scalar=rstd[:, jj : jj + 1],
-                        in1=b_ps[:, 0 : b - a],
-                        op0=ALU.mult,
-                        op1=ALU.add,
-                    )
+                nc.vector.scalar_tensor_tensor(
+                    out=o[:, jj * D : (jj + 1) * D],
+                    in0=o[:, jj * D : (jj + 1) * D],
+                    scalar=rstd[:, jj : jj + 1],
+                    in1=b_ps[:],
+                    op0=ALU.mult,
+                    op1=ALU.add,
+                )
             nc.sync.dma_start(out=out_view[:, c * GW : (c + 1) * GW], in_=o[:])
 
         expand_head_weights(0)
@@ -345,10 +344,19 @@ def tile_crossmodalattention_pa_t_kernel(
         ob_ps = spread(2, "kvT", "ob_ps")
         ob_sb = const.tile([P, D], BF16, name="ob_sb")
         nc.scalar.copy(out=ob_sb[:], in_=ob_ps[:])
+        obT = psum.tile([P, D], BF16, name="obT", tag="g_ps")
+        for n in range(4):
+            nc.tensor.transpose(
+                obT[:, n * P : (n + 1) * P], rows[:, 2 * D + n * P : 2 * D + (n + 1) * P], ident_b[:]
+            )
+        ob_cols = const.tile([P, D], F32, name="ob_cols")
+        nc.scalar.copy(
+            out=ob_cols[:].rearrange("p (n m) -> p n m", n=4),
+            in_=obT[:].rearrange("p (n m) -> p n m", n=4)[:, :, 0:1].to_broadcast([P, 4, P]),
+        )
         g_ps = spread(0, "g_ps", "g_ps")
         b_ps = spread(1, "b_ps", "b_ps")
         ow_f = ow_sb[:].bitcast(F32).rearrange("n (nb q a) -> n nb a q", nb=4, a=2)
-        b_sb = const.tile([P, GW], F32, name="b_sb")
 
         for tick in range(NG + 5):
             if tick % 4 == 0 and tick // 4 + 3 < len(chunks):
@@ -360,8 +368,10 @@ def tile_crossmodalattention_pa_t_kernel(
                 head_weights((tick + 2) // 4)
             if (tick + 3) % 4 == 0 and (tick + 3) // 4 < NT // BLK:
                 expand_head_weights((tick + 3) // 4)
+            if 0 <= tick - 1 < NG:
+                weigh_heads(tick - 1)
             if tick < NG:
-                residual(tick)
+                residual_gpsimd(tick)
             if tick < NG + 2:
                 quantise(tick)
             if tick < NG:
@@ -375,11 +385,9 @@ def tile_crossmodalattention_pa_t_kernel(
             if 0 <= tick - 3 < NG:
                 centre(tick - 3)
             if tick < NG:
-                weigh_heads(tick)
+                add_value_bias(tick)
+                residual_tensor(tick)
             if 0 <= tick - 2 < NG:
                 add_residual(tick - 2)
             if tick == 0:
                 og = weight_words(lambda nb, a: ow_f[:, nb, a, :], ("s2a", "s2b"), "o")
-                b2_ps = spread(1, "awT", "b2_ps")
-                for jj in range(GT):
-                    nc.scalar.copy(out=b_sb[:, jj * D : (jj + 1) * D], in_=b2_ps[:])

@@ -242,9 +242,12 @@ def tile_crossmodalattention_pa_t_kernel(
             attn = to_quantise(c + 2)[:, 4 * GC : 8 * GC]
             nc.vector.memset(attn[:, 0:2], 0.0)
             nc.gpsimd.tensor_tensor(
-                out=attn.rearrange("p (n t) -> p n t", t=4),
-                in0=st["planes", c][:].rearrange("p (t n) -> p n t", t=4),
-                in1=awE[:, lo : lo + GC].unsqueeze(2).to_broadcast([P, GC, 4]),
+                out=attn.rearrange("p (c i t) -> p c t i", i=4, t=4),
+                in0=st["planes", c][:].rearrange("p (t c i) -> p c t i", t=4, i=4),
+                in1=awE[:, lo : lo + GC]
+                .rearrange("p (c i) -> p c i", i=4)
+                .unsqueeze(2)
+                .to_broadcast([P, GC // 4, 4, 4]),
                 op=ALU.mult,
             )
 

@@ -20,9 +20,10 @@ NG = NT // GT
 GW = GT * D
 GC = GT * P
 BLK = 8
+NB = NT // BLK
 LN_EPS = 1e-5
 FLOPS = 2 * 2 * B * D * D
-PINNED = True
+TENSOR_COLS = 768
 
 
 def tile_crossmodalattention_pa_t_kernel(
@@ -30,8 +31,7 @@ def tile_crossmodalattention_pa_t_kernel(
 ):
     nc = tc.nc
     with ExitStack() as ctx:
-        if PINNED:
-            ctx.enter_context(tc.manual_schedule())
+        ctx.enter_context(tc.manual_schedule())
         const = ctx.enter_context(tc.tile_pool(name="const", bufs=1))
         w2 = ctx.enter_context(tc.tile_pool(name="w2", bufs=2))
         w3 = ctx.enter_context(tc.tile_pool(name="w3", bufs=3))
@@ -42,35 +42,30 @@ def tile_crossmodalattention_pa_t_kernel(
         q_view = q_in.rearrange("(p j) k -> p (j k)", j=NT)
         out_view = out.rearrange("(p j) n -> p (j n)", j=NT)
 
-        chunks = [(0, 2), (2, 8)] + [(a, a + 8) for a in range(8, NT, 8)]
+        chunks = [(0, 2), (2, 4), (4, 8)] + [(a, a + 8) for a in range(8, NT, 8)]
         kv_tiles = {}
         q_tiles = {}
+        st = {}
 
         def load_chunk(view, store, prefix, k):
+            if k >= len(chunks):
+                return
             j0, j1 = chunks[k]
-            t = const.tile([P, (j1 - j0) * D], BF16, name="%s%d" % (prefix, k))
+            if j1 - j0 < 8:
+                t = const.tile([P, (j1 - j0) * D], BF16, name="%s%d" % (prefix, k))
+            else:
+                t = w3.tile([P, (j1 - j0) * D], BF16, name=prefix + "s", tag=prefix + "s")
             nc.sync.dma_start(out=t[:], in_=view[:, j0 * D : j1 * D])
             for j in range(j0, j1):
                 store[j] = (t, (j - j0) * D)
 
-        eps = const.tile([P, 1], F32, name="eps")
-        nc.vector.memset(eps[:], LN_EPS)
-        warm = const.tile([P, 1], F32, name="warm")
-        nc.scalar.activation(out=warm[:], in_=eps[:], func=ACT.Abs_reciprocal_sqrt)
-        rows = const.tile([P, 3 * D], BF16, name="rows")
-        nc.vector.memset(rows[:], 0.0)
-        ones = const.tile([P, P], BF16, name="ones")
-        nc.vector.memset(ones[:], 1.0)
-        ident_f = const.tile([P, P], F32, name="ident_f")
-        make_identity(nc, ident_f[:])
-        ident_b = const.tile([P, P], BF16, name="ident_b")
-        make_identity(nc, ident_b[:])
-
         load_chunk(kv_view, kv_tiles, "kv", 0)
-        aw_sb = const.tile([P, NT * 8], BF16, name="aw_sb")
-        nc.sync.dma_start(out=aw_sb[:], in_=attn_w.rearrange("(p j) h o -> p (j h o)", j=NT))
         w_sb = const.tile([P, 4 * D], BF16, name="w_sb")
         nc.sync.dma_start(out=w_sb[:], in_=w_v.rearrange("(p t) k -> p (t k)", t=4))
+        aw_sb = const.tile([P, NT * 8], BF16, name="aw_sb")
+        nc.sync.dma_start(out=aw_sb[:], in_=attn_w.rearrange("(p j) h o -> p (j h o)", j=NT))
+        rows = const.tile([P, 3 * D], BF16, name="rows")
+        nc.gpsimd.memset(rows[:], 0.0)
         bv_bf = const.tile([P, 4], BF16, name="bv_bf")
         nc.sync.dma_start(out=bv_bf[:], in_=b_v.rearrange("(p t) -> p t", t=4))
         for i, vec in enumerate((ln_g, ln_b, out_b)):
@@ -83,14 +78,24 @@ def tile_crossmodalattention_pa_t_kernel(
             in_=out_w.rearrange("(nb p) d -> p nb d", p=P),
         )
         load_chunk(q_view, q_tiles, "q", 0)
-        load_chunk(kv_view, kv_tiles, "kv", 1)
-        load_chunk(q_view, q_tiles, "q", 1)
-        load_chunk(kv_view, kv_tiles, "kv", 2)
-        load_chunk(q_view, q_tiles, "q", 2)
+        for i in range(1, 4):
+            load_chunk(kv_view, kv_tiles, "kv", i)
+            load_chunk(q_view, q_tiles, "q", i)
 
-        def weight_words(words, tags, prefix):
-            grouped = const.tile([P, 4 * D], BF16, name=prefix + "g", align_bytes=64)
-            grouped_f = grouped[:].bitcast(F32)
+        eps = const.tile([P, 1], F32, name="eps")
+        nc.vector.memset(eps[:], LN_EPS)
+        warm = const.tile([P, 1], F32, name="warm")
+        nc.scalar.activation(out=warm[:], in_=eps[:], func=ACT.Abs_reciprocal_sqrt)
+        ones = const.tile([P, P], BF16, name="ones")
+        nc.vector.memset(ones[:], 1.0)
+        ident_f = const.tile([P, P], F32, name="ident_f")
+        make_identity(nc, ident_f[:])
+        ident_b = const.tile([P, P], BF16, name="ident_b")
+        nc.vector.tensor_copy(out=ident_b[:], in_=ident_f[:])
+        awE = const.tile([P, NT * P], BF16, name="awE")
+
+        def weight_banks(words, tags, prefix):
+            banks = []
             for b in range(2):
                 bank = psum.tile([P, D], F32, name=prefix + "T%d" % b, tag=tags[b])
                 for s in range(2):
@@ -100,13 +105,16 @@ def tile_crossmodalattention_pa_t_kernel(
                             words(2 * b + s, h),
                             ident_f[:],
                         )
-                nc.scalar.copy(
-                    out=grouped_f[:, b * D : (b + 1) * D].rearrange(
-                        "w (s c h) -> w s c h", s=2, h=2
-                    ),
-                    in_=bank[:].rearrange("w (s h c) -> w s c h", s=2, h=2),
-                )
-            return grouped
+                banks.append(bank)
+            return banks
+
+        def weight_out(banks, b, grouped, copy):
+            copy(
+                out=grouped[:].bitcast(F32)[:, b * D : (b + 1) * D].rearrange(
+                    "w (s c h) -> w s c h", s=2, h=2
+                ),
+                in_=banks[b][:].rearrange("w (s h c) -> w s c h", s=2, h=2),
+            )
 
         def quantise_weight(grouped, prefix):
             codes = const.tile([P, D], U32, name=prefix + "c", align_bytes=64)
@@ -121,70 +129,83 @@ def tile_crossmodalattention_pa_t_kernel(
             )
             return bank
 
-        st = {}
-
-        def expand_head_weights(blk):
+        def widen_head_weights(j0, j1, copy):
             awx = w2.tile([P, BLK * P], BF16, name="awx", tag="awx")
-            nc.scalar.copy(
-                out=awx[:].rearrange("p (m r) -> p m r", r=16),
-                in_=aw_sb[:, blk * 64 : (blk + 1) * 64].unsqueeze(2).to_broadcast([P, 64, 16]),
+            copy(
+                out=awx[:, 0 : (j1 - j0) * P].rearrange("p (m r) -> p m r", r=16),
+                in_=aw_sb[:, j0 * 8 : j1 * 8].unsqueeze(2).to_broadcast([P, (j1 - j0) * 8, 16]),
             )
-            st["awx", blk] = awx
+            st["awx", j0] = awx
 
-        def head_weights(blk):
-            awx = st["awx", blk]
-            awT = psum.tile([P, BLK * P], BF16, name="awT", tag="awT")
-            for j in range(BLK):
+        def transpose_head_weights(j0, j1, tag="kvT"):
+            awx = st["awx", j0]
+            awT = psum.tile([P, BLK * P], BF16, name="awT", tag=tag)
+            for j in range(j1 - j0):
                 nc.tensor.transpose(
                     awT[:, j * P : (j + 1) * P], awx[:, j * P : (j + 1) * P], ident_b[:]
                 )
-            awE = w2.tile([P, BLK * P], BF16, name="awE", tag="awE")
-            nc.scalar.copy(out=awE[:], in_=awT[:])
-            st["awE", blk] = awE
+            st["awT", j0] = awT
 
-        def residual_tensor(c):
+        def copy_head_weights(j0, j1, copy):
+            copy(out=awE[:, j0 * P : j1 * P], in_=st["awT", j0][:, 0 : (j1 - j0) * P])
+
+        def residual_tensor(c, lo, hi):
             t, off = q_tiles[GT * c]
-            bank = psum.tile([P, D], F32, name="qb", tag="awT")
+            bank = psum.tile([P, D], F32, name="qb", tag="qb")
             nc.tensor.matmul(
-                out=bank[:], lhsT=ident_b[:], rhs=t[:, off : off + D], start=True, stop=False
+                out=bank[:, 0 : hi - lo],
+                lhsT=ident_b[:],
+                rhs=t[:, off + lo : off + hi],
+                start=True,
+                stop=False,
             )
-            for n in range(4):
+            for n in range(0, hi - lo, P):
                 nc.tensor.matmul(
-                    out=bank[:, n * P : (n + 1) * P],
-                    lhsT=ob_cols[:, n * P : (n + 1) * P],
+                    out=bank[:, n : n + P],
+                    lhsT=ob_cols[:, n : n + P],
                     rhs=ident_f[:],
                     is_transpose=True,
                     start=False,
-                    stop=n == 3,
+                    stop=n + P == hi - lo,
                 )
-            qp0 = w3.tile([P, D], F32, name="qp0", tag="qp0")
-            nc.scalar.copy(out=qp0[:], in_=bank[:])
-            st["qp", c, 0] = qp0
+            st["qb", c, lo] = (bank, hi)
+
+        def residual_out(c, lo):
+            bank, hi = st["qb", c, lo]
+            if ("qp", c) not in st:
+                st["qp", c] = w3.tile([P, GW], F32, name="qp", tag="qp")
+            nc.scalar.copy(out=st["qp", c][:, lo:hi], in_=bank[:, 0 : hi - lo])
 
         def residual_gpsimd(c):
-            qp1 = w3.tile([P, D], F32, name="qp1", tag="qp1")
-            t, off = q_tiles[GT * c + 1]
+            t, off = q_tiles[GT * c]
+            if ("qp", c) not in st:
+                st["qp", c] = w3.tile([P, GW], F32, name="qp", tag="qp")
             nc.gpsimd.tensor_tensor(
-                out=qp1[:], in0=t[:, off : off + D], in1=ob_sb[:], op=ALU.add
+                out=st["qp", c][:, TENSOR_COLS:GW],
+                in0=t[:, off + TENSOR_COLS : off + GW],
+                in1=ob_sb[:, TENSOR_COLS - D : D],
+                op=ALU.add,
             )
-            st["qp", c, 1] = qp1
 
-        def to_quantise(tick):
-            if ("qin", tick) not in st:
-                st["qin", tick] = w3.tile([P, 8 * GC], BF16, name="qin", tag="qin", align_bytes=64)
-            return st["qin", tick]
+        def qin(k):
+            if ("qin", k) not in st:
+                st["qin", k] = w3.tile([P, 8 * GC], BF16, name="qin", tag="qin", align_bytes=64)
+            return st["qin", k]
 
-        def quantise(tick):
-            lo = 0 if tick < NG else GC
-            hi = 2 * GC if tick >= 2 else GC
-            codes = w2.tile([P, 2 * GC], U32, name="codes", tag="codes", align_bytes=64)
-            scales = w2.tile([P, 2 * GC], U8, name="scales", tag="scales", align_bytes=64)
+        def attn_half(c):
+            return qin(c + 2)[:, 4 * GC : 8 * GC]
+
+        def quantise(k, lo, hi):
+            if ("codes", k) not in st:
+                codes = w2.tile([P, 2 * GC], U32, name="codes", tag="codes", align_bytes=64)
+                scales = w2.tile([P, 2 * GC], U8, name="scales", tag="scales", align_bytes=64)
+                st["codes", k] = (codes, scales)
+            codes, scales = st["codes", k]
             nc.vector.quantize_mx(
                 out=codes[:, lo:hi].bitcast(FP8X4),
                 scales=scales[:, lo:hi],
-                in_=to_quantise(tick)[:, 4 * lo : 4 * hi],
+                in_=qin(k)[:, 4 * lo : 4 * hi],
             )
-            st["codes", tick] = (codes, scales)
 
         def transpose_kv(c):
             kvT = psum.tile([P, D], F32, name="kvT", tag="kvT")
@@ -198,11 +219,14 @@ def tile_crossmodalattention_pa_t_kernel(
                         t_f[:, lo + u : lo + 2 * P : 2],
                         ident_f[:],
                     )
-            nc.scalar.copy(
-                out=to_quantise(c)[:, 0 : 4 * GC]
+            st["kvT", c] = kvT
+
+        def copy_kv(c, copy):
+            copy(
+                out=qin(c)[:, 0 : 4 * GC]
                 .bitcast(F32)
                 .rearrange("w (s c h) -> w s c h", s=GT, h=2),
-                in_=kvT[:].rearrange("w (s h c) -> w s c h", s=GT, h=2),
+                in_=st["kvT", c][:].rearrange("w (s h c) -> w s c h", s=GT, h=2),
             )
 
         def first_matmul(c):
@@ -236,13 +260,31 @@ def tile_crossmodalattention_pa_t_kernel(
                 )
             st["planes", c] = planes
 
-        def weigh_heads(c):
-            awE = st["awE", (GT * c) // BLK]
-            lo = ((GT * c) % BLK) * P
-            attn = to_quantise(c + 2)[:, 4 * GC : 8 * GC]
-            nc.vector.memset(attn[:, 0:2], 0.0)
-            nc.gpsimd.tensor_tensor(
-                out=attn.rearrange("p (c i t) -> p c t i", i=4, t=4),
+        def weigh_heads_vector(c):
+            banks = st["s1", c]
+            lo = GT * c * P
+            planes = w2.tile([P, 4 * GC], BF16, name="planes_v", tag="planes")
+            for t in range(4):
+                nc.vector.scalar_tensor_tensor(
+                    out=planes[:, t * GC : (t + 1) * GC],
+                    in0=banks[t // 2][:, (t % 2) * GC : (t % 2 + 1) * GC],
+                    scalar=bv[:, t : t + 1],
+                    in1=awE[:, lo : lo + GC],
+                    op0=ALU.add,
+                    op1=ALU.mult,
+                )
+            st["planes_v", c] = planes
+
+        def interleave(c, copy):
+            copy(
+                out=attn_half(c).rearrange("p (c i t) -> p c t i", i=4, t=4),
+                in_=st["planes_v", c][:].rearrange("p (t c i) -> p c t i", t=4, i=4),
+            )
+
+        def weigh_heads(c, engine):
+            lo = GT * c * P
+            engine.tensor_tensor(
+                out=attn_half(c).rearrange("p (c i t) -> p c t i", i=4, t=4),
                 in0=st["planes", c][:].rearrange("p (t c i) -> p c t i", t=4, i=4),
                 in1=awE[:, lo : lo + GC]
                 .rearrange("p (c i) -> p c i", i=4)
@@ -250,6 +292,10 @@ def tile_crossmodalattention_pa_t_kernel(
                 .to_broadcast([P, GC // 4, 4, 4]),
                 op=ALU.mult,
             )
+
+        def release_gpsimd(c):
+            first = 0 if c + 1 < NG else 4 * GC
+            nc.vector.tensor_copy(out=attn_half(c)[:, 0:1], in_=qin(c + 1)[:, first : first + 1])
 
         def second_matmul(c):
             codes, scales = st["codes", c + 2]
@@ -272,31 +318,42 @@ def tile_crossmodalattention_pa_t_kernel(
         def add_residual(c):
             banks = st["s2", c]
             z = w2.tile([P, GW], F32, name="z", tag="z")
-            sums = w2.tile([P, GT], F32, name="sums", tag="sums")
+            sums = w3.tile([P, GT], F32, name="sums", tag="sums")
             for jj in range(GT):
                 nc.vector.scalar_tensor_tensor(
                     out=z[:, jj * D : (jj + 1) * D],
                     in0=banks[jj][:],
                     scalar=0.0,
-                    in1=st["qp", c, jj][:],
+                    in1=st["qp", c][:, jj * D : (jj + 1) * D],
                     op0=ALU.add,
                     op1=ALU.add,
                     accum_out=sums[:, jj : jj + 1],
                 )
-            negmu = w2.tile([P, GT], F32, name="negmu", tag="negmu")
+            st["z", c] = (z, sums)
+
+        def means(c):
+            z, sums = st["z", c]
+            negmu = w3.tile([P, GT], F32, name="negmu", tag="negmu")
             nc.scalar.mul(out=negmu[:], in_=sums[:], mul=-1.0 / D)
-            ssq = w2.tile([P, GT], F32, name="ssq", tag="ssq")
-            for jj in range(GT):
-                junk = w2.tile([P, D], BF16, name="junk", tag="junk")
-                nc.scalar.activation(
-                    out=junk[:],
-                    in_=z[:, jj * D : (jj + 1) * D],
-                    func=ACT.Square,
-                    bias=negmu[:, jj : jj + 1],
-                    scale=1.0,
-                    accum_out=ssq[:, jj : jj + 1],
-                )
-            rstd = w2.tile([P, GT], F32, name="rstd", tag="rstd")
+            ssq = w3.tile([P, GT], F32, name="ssq", tag="ssq")
+            st["stat", c] = (negmu, ssq)
+
+        def square(c, jj):
+            z, sums = st["z", c]
+            negmu, ssq = st["stat", c]
+            junk = w2.tile([P, D], BF16, name="junk", tag="junk")
+            nc.scalar.activation(
+                out=junk[:],
+                in_=z[:, jj * D : (jj + 1) * D],
+                func=ACT.Square,
+                bias=negmu[:, jj : jj + 1],
+                scale=1.0,
+                accum_out=ssq[:, jj : jj + 1],
+            )
+
+        def deviation(c):
+            negmu, ssq = st["stat", c]
+            rstd = w3.tile([P, GT], F32, name="rstd", tag="rstd")
             nc.scalar.activation(
                 out=rstd[:],
                 in_=ssq[:],
@@ -304,10 +361,11 @@ def tile_crossmodalattention_pa_t_kernel(
                 bias=eps[:, 0:1],
                 scale=1.0 / D,
             )
-            st["z", c] = (z, negmu, rstd)
+            st["rstd", c] = rstd
 
         def centre(c):
-            z, negmu, rstd = st["z", c]
+            z, sums = st["z", c]
+            negmu, ssq = st["stat", c]
             o = w4.tile([P, GW], F32, name="o", tag="o")
             for jj in range(GT):
                 nc.vector.scalar_tensor_tensor(
@@ -320,77 +378,154 @@ def tile_crossmodalattention_pa_t_kernel(
                 )
             st["o", c] = o
 
-        def finish(c):
-            z, negmu, rstd = st["z", c]
+        def finish(c, jj):
+            rstd = st["rstd", c]
             o = st["o", c]
-            for jj in range(GT):
-                nc.vector.scalar_tensor_tensor(
-                    out=o[:, jj * D : (jj + 1) * D],
-                    in0=o[:, jj * D : (jj + 1) * D],
-                    scalar=rstd[:, jj : jj + 1],
-                    in1=b_ps[:],
-                    op0=ALU.mult,
-                    op1=ALU.add,
-                )
-            nc.sync.dma_start(out=out_view[:, c * GW : (c + 1) * GW], in_=o[:])
+            nc.vector.scalar_tensor_tensor(
+                out=o[:, jj * D : (jj + 1) * D],
+                in0=o[:, jj * D : (jj + 1) * D],
+                scalar=rstd[:, jj : jj + 1],
+                in1=b_ps[:],
+                op0=ALU.mult,
+                op1=ALU.add,
+            )
 
-        expand_head_weights(0)
-        transpose_kv(0)
+        def store(c, lo=0, hi=GW):
+            nc.sync.dma_start(
+                out=out_view[:, c * GW + lo : c * GW + hi], in_=st["o", c][:, lo:hi]
+            )
+
+        vcopy = nc.vector.tensor_copy
+        scopy = nc.scalar.copy
         w_f = w_sb[:].bitcast(F32)
-        wg = weight_words(
-            lambda t, u: w_f[:, t * 256 + u : (t + 1) * 256 : 2], ("s1a", "s1b"), "w"
-        )
-        wc, ws = quantise_weight(wg, "w")
-        head_weights(0)
+        ow_f = ow_sb[:].bitcast(F32).rearrange("n (nb q a) -> n nb a q", nb=4, a=2)
         bv = const.tile([P, 4], F32, name="bv")
-        nc.vector.tensor_copy(out=bv[:], in_=bv_bf[:])
-        ob_ps = spread(2, "kvT", "ob_ps")
+        wg = const.tile([P, 4 * D], BF16, name="wg", align_bytes=64)
+        og = const.tile([P, 4 * D], BF16, name="og", align_bytes=64)
+        ob_cols = const.tile([P, D], F32, name="ob_cols")
         ob_sb = const.tile([P, D], BF16, name="ob_sb")
-        nc.scalar.copy(out=ob_sb[:], in_=ob_ps[:])
-        obT = psum.tile([P, D], BF16, name="obT", tag="g_ps")
+
+        transpose_kv(0)
+        copy_kv(0, scopy)
+        w_banks = weight_banks(lambda t, u: w_f[:, t * 256 + u : (t + 1) * 256 : 2], ("s1a", "s1b"), "w")
+        widen_head_weights(0, 8, vcopy)
+        quantise(0, 0, GC)
+        widen_head_weights(8, 16, vcopy)
+        weight_out(w_banks, 0, wg, scopy)
+        weight_out(w_banks, 1, wg, vcopy)
+        transpose_head_weights(0, 8, "qb")
+        obT = psum.tile([P, D], BF16, name="obT", tag="b_ps")
         for n in range(4):
             nc.tensor.transpose(
                 obT[:, n * P : (n + 1) * P], rows[:, 2 * D + n * P : 2 * D + (n + 1) * P], ident_b[:]
             )
-        ob_cols = const.tile([P, D], F32, name="ob_cols")
+        ob_ps = spread(2, "g_ps", "ob_ps")
         nc.scalar.copy(
             out=ob_cols[:].rearrange("p (n m) -> p n m", n=4),
             in_=obT[:].rearrange("p (n m) -> p n m", n=4)[:, :, 0:1].to_broadcast([P, 4, P]),
         )
-        g_ps = spread(0, "g_ps", "g_ps")
+        nc.scalar.copy(out=ob_sb[:], in_=ob_ps[:])
+        o_banks = weight_banks(lambda nb, a: ow_f[:, nb, a, :], ("s2a", "s2b"), "o")
+        wc, ws = quantise_weight(wg, "w")
+        nc.vector.tensor_copy(out=bv[:], in_=bv_bf[:])
+        copy_head_weights(0, 8, vcopy)
+        first_matmul(0)
+        transpose_kv(1)
+        transpose_head_weights(8, 16, "b_ps")
+        residual_tensor(0, 0, D)
+        weight_out(o_banks, 0, og, scopy)
+        weight_out(o_banks, 1, og, scopy)
+        copy_kv(1, scopy)
+        transpose_kv(2)
+        residual_out(0, 0)
+        residual_tensor(0, D, TENSOR_COLS)
+        residual_gpsimd(0)
+        residual_gpsimd(1)
+        weigh_heads_vector(0)
+        oc, os_ = quantise_weight(og, "o")
+        interleave(0, scopy)
+        copy_head_weights(8, 16, vcopy)
+        quantise(1, 0, GC)
+        first_matmul(1)
+        residual_out(0, D)
+        quantise(2, GC, 2 * GC)
+        second_matmul(0)
+        residual_tensor(1, 0, D)
+        weigh_heads_vector(1)
+        copy_kv(2, scopy)
+        transpose_kv(3)
+        residual_out(1, 0)
+        residual_tensor(1, D, TENSOR_COLS)
+        add_residual(0)
+        interleave(1, scopy)
+        residual_out(1, D)
+        quantise(2, 0, GC)
+        first_matmul(2)
+        residual_gpsimd(2)
         b_ps = spread(1, "b_ps", "b_ps")
-        ow_f = ow_sb[:].bitcast(F32).rearrange("n (nb q a) -> n nb a q", nb=4, a=2)
+        g_ps = spread(0, "g_ps", "g_ps")
+        means(0)
+        quantise(3, GC, 2 * GC)
+        second_matmul(1)
+        add_value_bias(2)
+        square(0, 0)
+        square(0, 1)
+        residual_tensor(2, 0, D)
+        copy_kv(3, scopy)
+        transpose_kv(4)
+        deviation(0)
+        centre(0)
+        add_residual(1)
+        weigh_heads(2, nc.gpsimd)
+        residual_gpsimd(3)
+        residual_out(2, 0)
+        residual_tensor(2, D, TENSOR_COLS)
+        quantise(3, 0, GC)
+        first_matmul(3)
+        means(1)
+        square(1, 0)
+        square(1, 1)
+        residual_out(2, D)
+        residual_tensor(3, 0, D)
+        deviation(1)
+        copy_kv(4, scopy)
+        finish(0, 0)
+        finish(0, 1)
+        store(0)
+        centre(1)
+        add_value_bias(3)
+        residual_out(3, 0)
+        residual_tensor(3, D, TENSOR_COLS)
+        residual_out(3, D)
 
-        for tick in range(NG + 5):
-            if tick % 4 == 0 and tick // 4 + 3 < len(chunks):
+        def at(lag, fn, *args):
+            if tick - lag < NG:
+                fn(tick - lag, *args)
+
+        for tick in range(4, NG + 6):
+            if tick % 4 == 0:
                 load_chunk(kv_view, kv_tiles, "kv", tick // 4 + 3)
                 load_chunk(q_view, q_tiles, "q", tick // 4 + 3)
-            if tick + 1 < NG:
-                transpose_kv(tick + 1)
-            if (tick + 2) % 4 == 0 and (tick + 2) // 4 < NT // BLK:
-                head_weights((tick + 2) // 4)
-            if (tick + 3) % 4 == 0 and (tick + 3) // 4 < NT // BLK:
-                expand_head_weights((tick + 3) // 4)
-            if 0 <= tick - 1 < NG:
-                weigh_heads(tick - 1)
-            if tick < NG:
-                residual_gpsimd(tick)
-            if tick < NG + 2:
-                quantise(tick)
-            if tick < NG:
-                first_matmul(tick)
-            if tick == 1:
-                oc, os_ = quantise_weight(og, "o")
-            if 0 <= tick - 2 < NG:
-                second_matmul(tick - 2)
-            if 0 <= tick - 4 < NG:
-                finish(tick - 4)
-            if 0 <= tick - 3 < NG:
-                centre(tick - 3)
-            if tick < NG:
-                add_value_bias(tick)
-                residual_tensor(tick)
-            if 0 <= tick - 2 < NG:
-                add_residual(tick - 2)
-            if tick == 0:
-                og = weight_words(lambda nb, a: ow_f[:, nb, a, :], ("s2a", "s2b"), "o")
+            if tick + 1 < NG: transpose_kv(tick + 1)
+            if tick - 1 < NG: release_gpsimd(tick - 1); weigh_heads(tick - 1, nc.gpsimd)
+            if tick < NG: residual_gpsimd(tick)
+            if tick < NG + 2: quantise(tick, 0 if tick < NG else GC, 2 * GC)
+            at(0, first_matmul)
+            at(2, second_matmul)
+            if tick == 4: residual_tensor(4, 0, D)
+            if tick > 4 and tick - 4 < NG: finish(tick - 4, 0); finish(tick - 4, 1); store(tick - 4)
+            if tick > 4: at(3, centre)
+            if tick + 1 < NG: copy_kv(tick + 1, scopy)
+            at(0, residual_out, 0)
+            if tick > 4: at(3, deviation)
+            at(0, residual_tensor, D, TENSOR_COLS)
+            if tick % 2 == 1 and 3 < tick and 2 * tick + 6 < NT: transpose_head_weights(2 * tick + 6, 2 * tick + 10)
+            at(0, add_value_bias)
+            at(0, residual_out, D)
+            if tick % 2 == 1 and 3 < tick and 2 * tick + 6 < NT: copy_head_weights(2 * tick + 6, 2 * tick + 10, scopy)
+            at(2, add_residual)
+            at(2, means)
+            if tick + 1 < NG: residual_tensor(tick + 1, 0, D)
+            if tick % 2 == 0 and 2 * tick + 8 < NT: widen_head_weights(2 * tick + 8, 2 * tick + 12, scopy)
+            at(2, square, 0)
+            at(2, square, 1)

@@ -94,26 +94,23 @@ def tile_crossmodalattention_pa_t_kernel(
         nc.vector.tensor_copy(out=ident_b[:], in_=ident_f[:])
         awE = const.tile([P, NT * P], BF16, name="awE")
 
-        def weight_banks(words, tags, prefix):
-            banks = []
-            for b in range(2):
-                bank = psum.tile([P, D], F32, name=prefix + "T%d" % b, tag=tags[b])
-                for s in range(2):
-                    for h in range(2):
-                        nc.tensor.transpose(
-                            bank[:, (s * 2 + h) * P : (s * 2 + h + 1) * P],
-                            words(2 * b + s, h),
-                            ident_f[:],
-                        )
-                banks.append(bank)
-            return banks
+        def transpose_weight(words, b, tag, prefix):
+            bank = psum.tile([P, D], F32, name=prefix + "T%d" % b, tag=tag)
+            for s in range(2):
+                for h in range(2):
+                    nc.tensor.transpose(
+                        bank[:, (s * 2 + h) * P : (s * 2 + h + 1) * P],
+                        words(2 * b + s, h),
+                        ident_f[:],
+                    )
+            return bank
 
-        def weight_out(banks, b, grouped, copy):
+        def weight_out(bank, b, grouped, copy):
             copy(
                 out=grouped[:].bitcast(F32)[:, b * D : (b + 1) * D].rearrange(
                     "w (s c h) -> w s c h", s=2, h=2
                 ),
-                in_=banks[b][:].rearrange("w (s h c) -> w s c h", s=2, h=2),
+                in_=bank[:].rearrange("w (s h c) -> w s c h", s=2, h=2),
             )
 
         def quantise_weight(grouped, prefix):
@@ -149,9 +146,9 @@ def tile_crossmodalattention_pa_t_kernel(
         def copy_head_weights(j0, j1, copy):
             copy(out=awE[:, j0 * P : j1 * P], in_=st["awT", j0][:, 0 : (j1 - j0) * P])
 
-        def residual_tensor(c, lo, hi):
+        def residual_tensor(c, lo, hi, tag="qb"):
             t, off = q_tiles[GT * c]
-            bank = psum.tile([P, D], F32, name="qb", tag="qb")
+            bank = psum.tile([P, D], F32, name="qb", tag=tag)
             nc.tensor.matmul(
                 out=bank[:, 0 : hi - lo],
                 lhsT=ident_b[:],
@@ -407,12 +404,19 @@ def tile_crossmodalattention_pa_t_kernel(
 
         transpose_kv(0)
         copy_kv(0, scopy)
-        w_banks = weight_banks(lambda t, u: w_f[:, t * 256 + u : (t + 1) * 256 : 2], ("s1a", "s1b"), "w")
+        def w_words(t, u):
+            return w_f[:, t * 256 + u : (t + 1) * 256 : 2]
+
+        def ow_words(nb, a):
+            return ow_f[:, nb, a, :]
+
+        w_a = transpose_weight(w_words, 0, "s1a", "w")
+        w_b = transpose_weight(w_words, 1, "s1b", "w")
         widen_head_weights(0, 8, vcopy)
         quantise(0, 0, GC)
         widen_head_weights(8, 16, vcopy)
-        weight_out(w_banks, 0, wg, scopy)
-        weight_out(w_banks, 1, wg, vcopy)
+        weight_out(w_a, 0, wg, scopy)
+        weight_out(w_b, 1, wg, vcopy)
         transpose_head_weights(0, 8, "qb")
         obT = psum.tile([P, D], BF16, name="obT", tag="b_ps")
         for n in range(4):
@@ -425,16 +429,17 @@ def tile_crossmodalattention_pa_t_kernel(
             in_=obT[:].rearrange("p (n m) -> p n m", n=4)[:, :, 0:1].to_broadcast([P, 4, P]),
         )
         nc.scalar.copy(out=ob_sb[:], in_=ob_ps[:])
-        o_banks = weight_banks(lambda nb, a: ow_f[:, nb, a, :], ("s2a", "s2b"), "o")
         wc, ws = quantise_weight(wg, "w")
         nc.vector.tensor_copy(out=bv[:], in_=bv_bf[:])
         copy_head_weights(0, 8, vcopy)
         first_matmul(0)
+        o_a = transpose_weight(ow_words, 0, "s2a", "o")
+        o_b = transpose_weight(ow_words, 1, "s2b", "o")
         transpose_kv(1)
         transpose_head_weights(8, 16, "b_ps")
         residual_tensor(0, 0, D)
-        weight_out(o_banks, 0, og, scopy)
-        weight_out(o_banks, 1, og, scopy)
+        weight_out(o_a, 0, og, scopy)
+        weight_out(o_b, 1, og, scopy)
         copy_kv(1, scopy)
         transpose_kv(2)
         residual_out(0, 0)
@@ -506,26 +511,25 @@ def tile_crossmodalattention_pa_t_kernel(
             if tick % 4 == 0:
                 load_chunk(kv_view, kv_tiles, "kv", tick // 4 + 3)
                 load_chunk(q_view, q_tiles, "q", tick // 4 + 3)
-            if tick + 1 < NG: transpose_kv(tick + 1)
             if tick - 1 < NG: release_gpsimd(tick - 1); weigh_heads(tick - 1, nc.gpsimd)
             if tick < NG: residual_gpsimd(tick)
             if tick < NG + 2: quantise(tick, 0 if tick < NG else GC, 2 * GC)
             at(0, first_matmul)
+            if tick + 1 < NG: transpose_kv(tick + 1)
             at(2, second_matmul)
-            if tick == 4: residual_tensor(4, 0, D)
+            at(0, residual_tensor, 0, D)
             if tick > 4 and tick - 4 < NG: finish(tick - 4, 0); finish(tick - 4, 1); store(tick - 4)
             if tick > 4: at(3, centre)
-            if tick + 1 < NG: copy_kv(tick + 1, scopy)
-            at(0, residual_out, 0)
-            if tick > 4: at(3, deviation)
-            at(0, residual_tensor, D, TENSOR_COLS)
-            if tick % 2 == 1 and 3 < tick and 2 * tick + 6 < NT: transpose_head_weights(2 * tick + 6, 2 * tick + 10)
             at(0, add_value_bias)
-            at(0, residual_out, D)
-            if tick % 2 == 1 and 3 < tick and 2 * tick + 6 < NT: copy_head_weights(2 * tick + 6, 2 * tick + 10, scopy)
+            if tick > 4: at(3, deviation)
+            if tick + 1 < NG: copy_kv(tick + 1, scopy)
+            if tick % 2 == 0 and 2 * tick + 8 < NT: widen_head_weights(2 * tick + 8, 2 * tick + 12, scopy)
+            at(0, residual_tensor, D, TENSOR_COLS, "kvT")
+            at(0, residual_out, 0)
+            if tick % 2 == 1 and 3 < tick and 2 * tick + 6 < NT: transpose_head_weights(2 * tick + 6, 2 * tick + 10, "qb")
             at(2, add_residual)
             at(2, means)
-            if tick + 1 < NG: residual_tensor(tick + 1, 0, D)
-            if tick % 2 == 0 and 2 * tick + 8 < NT: widen_head_weights(2 * tick + 8, 2 * tick + 12, scopy)
+            at(0, residual_out, D)
+            if tick % 2 == 1 and 3 < tick and 2 * tick + 6 < NT: copy_head_weights(2 * tick + 6, 2 * tick + 10, scopy)
             at(2, square, 0)
             at(2, square, 1)

@@ -24,6 +24,7 @@ NB = NT // BLK
 LN_EPS = 1e-5
 FLOPS = 2 * 2 * B * D * D
 TENSOR_COLS = 768
+ENGINE_TILES = 16
 
 
 def tile_crossmodalattention_pa_t_kernel(
@@ -35,7 +36,7 @@ def tile_crossmodalattention_pa_t_kernel(
         const = ctx.enter_context(tc.tile_pool(name="const", bufs=1))
         w2 = ctx.enter_context(tc.tile_pool(name="w2", bufs=2))
         w3 = ctx.enter_context(tc.tile_pool(name="w3", bufs=3))
-        w4 = ctx.enter_context(tc.tile_pool(name="w4", bufs=4))
+        w4 = ctx.enter_context(tc.tile_pool(name="w4", bufs=6))
         psum = ctx.enter_context(tc.psum_pool(name="psum", bufs=1))
 
         kv_view = kv_in.rearrange("(p j) k -> p (j k)", j=NT)
@@ -92,7 +93,8 @@ def tile_crossmodalattention_pa_t_kernel(
         make_identity(nc, ident_f[:])
         ident_b = const.tile([P, P], BF16, name="ident_b")
         nc.vector.tensor_copy(out=ident_b[:], in_=ident_f[:])
-        awE = const.tile([P, NT * P], BF16, name="awE")
+        awE = const.tile([P, ENGINE_TILES * P], BF16, name="awE")
+        awF = const.tile([P, (NT - ENGINE_TILES) * P], F32, name="awF")
 
         def transpose_weight(words, b, tag, prefix):
             bank = psum.tile([P, D], F32, name=prefix + "T%d" % b, tag=tag)
@@ -143,6 +145,36 @@ def tile_crossmodalattention_pa_t_kernel(
                 )
             st["awT", j0] = awT
 
+        def spread_head_weights():
+            nblk = (NT - ENGINE_TILES) // 16
+            flat = out.rearrange("r n -> (r n)")
+            size = P * 16 * P
+            base = B * D - nblk * size
+            awT = psum.tile([P, nblk * P], BF16, name="awT2", tag="kvT")
+            for i in range(nblk):
+                lo = (ENGINE_TILES + 16 * i) * 8
+                nc.tensor.transpose(awT[:, i * P : (i + 1) * P], aw_sb[:, lo : lo + P], ident_b[:])
+            awS = const.tile([P, nblk * P], F32, name="awS")
+            nc.vector.tensor_copy(out=awS[:], in_=awT[:])
+            segs = [flat[base + i * size : base + (i + 1) * size] for i in range(nblk)]
+            for i in range(nblk):
+                nc.sync.dma_start(
+                    out=segs[i].rearrange("(q r p) -> q r p", r=16, p=P),
+                    in_=awS[:, i * P : (i + 1) * P].unsqueeze(1).to_broadcast([P, 16, P]),
+                )
+            for i in range(nblk):
+                nc.sync.dma_start(
+                    out=awF[:, i * 16 * P : (i + 1) * 16 * P].rearrange("q (j p) -> q j p", p=P),
+                    in_=segs[i].rearrange("(j q p) -> q j p", j=16, p=P),
+                )
+
+        def head_weights(c):
+            lo = GT * c * P
+            if GT * c < ENGINE_TILES:
+                return awE[:, lo : lo + GC]
+            lo -= ENGINE_TILES * P
+            return awF[:, lo : lo + GC]
+
         def copy_head_weights(j0, j1, copy):
             copy(out=awE[:, j0 * P : j1 * P], in_=st["awT", j0][:, 0 : (j1 - j0) * P])
 
@@ -167,11 +199,11 @@ def tile_crossmodalattention_pa_t_kernel(
                 )
             st["qb", c, lo] = (bank, hi)
 
-        def residual_out(c, lo):
+        def residual_out(c, lo, copy=nc.scalar.copy):
             bank, hi = st["qb", c, lo]
             if ("qp", c) not in st:
                 st["qp", c] = w3.tile([P, GW], F32, name="qp", tag="qp")
-            nc.scalar.copy(out=st["qp", c][:, lo:hi], in_=bank[:, 0 : hi - lo])
+            copy(out=st["qp", c][:, lo:hi], in_=bank[:, 0 : hi - lo])
 
         def residual_gpsimd(c):
             t, off = q_tiles[GT * c]
@@ -259,14 +291,13 @@ def tile_crossmodalattention_pa_t_kernel(
 
         def weigh_heads_vector(c):
             banks = st["s1", c]
-            lo = GT * c * P
             planes = w2.tile([P, 4 * GC], BF16, name="planes_v", tag="planes")
             for t in range(4):
                 nc.vector.scalar_tensor_tensor(
                     out=planes[:, t * GC : (t + 1) * GC],
                     in0=banks[t // 2][:, (t % 2) * GC : (t % 2 + 1) * GC],
                     scalar=bv[:, t : t + 1],
-                    in1=awE[:, lo : lo + GC],
+                    in1=head_weights(c),
                     op0=ALU.add,
                     op1=ALU.mult,
                 )
@@ -279,11 +310,10 @@ def tile_crossmodalattention_pa_t_kernel(
             )
 
         def weigh_heads(c, engine):
-            lo = GT * c * P
             engine.tensor_tensor(
                 out=attn_half(c).rearrange("p (c i t) -> p c t i", i=4, t=4),
                 in0=st["planes", c][:].rearrange("p (t c i) -> p c t i", t=4, i=4),
-                in1=awE[:, lo : lo + GC]
+                in1=head_weights(c)
                 .rearrange("p (c i) -> p c i", i=4)
                 .unsqueeze(2)
                 .to_broadcast([P, GC // 4, 4, 4]),
@@ -369,7 +399,7 @@ def tile_crossmodalattention_pa_t_kernel(
                     out=o[:, jj * D : (jj + 1) * D],
                     in0=z[:, jj * D : (jj + 1) * D],
                     scalar=negmu[:, jj : jj + 1],
-                    in1=g_ps[:],
+                    in1=gb_ps[:, 0:D],
                     op0=ALU.add,
                     op1=ALU.mult,
                 )
@@ -382,7 +412,7 @@ def tile_crossmodalattention_pa_t_kernel(
                 out=o[:, jj * D : (jj + 1) * D],
                 in0=o[:, jj * D : (jj + 1) * D],
                 scalar=rstd[:, jj : jj + 1],
-                in1=b_ps[:],
+                in1=gb_ps[:, D : 2 * D],
                 op0=ALU.mult,
                 op1=ALU.add,
             )
@@ -418,12 +448,13 @@ def tile_crossmodalattention_pa_t_kernel(
         weight_out(w_a, 0, wg, scopy)
         weight_out(w_b, 1, wg, vcopy)
         transpose_head_weights(0, 8, "qb")
-        obT = psum.tile([P, D], BF16, name="obT", tag="b_ps")
+        transpose_head_weights(8, 16, "kvT")
+        obT = psum.tile([P, D], BF16, name="obT", tag="qc")
         for n in range(4):
             nc.tensor.transpose(
                 obT[:, n * P : (n + 1) * P], rows[:, 2 * D + n * P : 2 * D + (n + 1) * P], ident_b[:]
             )
-        ob_ps = spread(2, "g_ps", "ob_ps")
+        ob_ps = spread(2, "gb", "ob_ps")
         nc.scalar.copy(
             out=ob_cols[:].rearrange("p (n m) -> p n m", n=4),
             in_=obT[:].rearrange("p (n m) -> p n m", n=4)[:, :, 0:1].to_broadcast([P, 4, P]),
@@ -432,24 +463,24 @@ def tile_crossmodalattention_pa_t_kernel(
         wc, ws = quantise_weight(wg, "w")
         nc.vector.tensor_copy(out=bv[:], in_=bv_bf[:])
         copy_head_weights(0, 8, vcopy)
+        copy_head_weights(8, 16, vcopy)
+        spread_head_weights()
         first_matmul(0)
         o_a = transpose_weight(ow_words, 0, "s2a", "o")
         o_b = transpose_weight(ow_words, 1, "s2b", "o")
         transpose_kv(1)
-        transpose_head_weights(8, 16, "b_ps")
         residual_tensor(0, 0, D)
         weight_out(o_a, 0, og, scopy)
         weight_out(o_b, 1, og, scopy)
         copy_kv(1, scopy)
         transpose_kv(2)
         residual_out(0, 0)
-        residual_tensor(0, D, TENSOR_COLS)
+        residual_tensor(0, D, TENSOR_COLS, "qc")
         residual_gpsimd(0)
         residual_gpsimd(1)
         weigh_heads_vector(0)
         oc, os_ = quantise_weight(og, "o")
         interleave(0, scopy)
-        copy_head_weights(8, 16, vcopy)
         quantise(1, 0, GC)
         first_matmul(1)
         residual_out(0, D)
@@ -460,15 +491,22 @@ def tile_crossmodalattention_pa_t_kernel(
         copy_kv(2, scopy)
         transpose_kv(3)
         residual_out(1, 0)
-        residual_tensor(1, D, TENSOR_COLS)
+        residual_tensor(1, D, TENSOR_COLS, "qc")
         add_residual(0)
         interleave(1, scopy)
         residual_out(1, D)
         quantise(2, 0, GC)
         first_matmul(2)
         residual_gpsimd(2)
-        b_ps = spread(1, "b_ps", "b_ps")
-        g_ps = spread(0, "g_ps", "g_ps")
+        gb_ps = psum.tile([P, 2 * D], BF16, name="gb_ps", tag="gb")
+        for i in range(2):
+            nc.tensor.matmul(
+                out=gb_ps[:, i * D : (i + 1) * D],
+                lhsT=ones[:],
+                rhs=rows[:, i * D : (i + 1) * D],
+                start=True,
+                stop=True,
+            )
         means(0)
         quantise(3, GC, 2 * GC)
         second_matmul(1)
@@ -484,7 +522,7 @@ def tile_crossmodalattention_pa_t_kernel(
         weigh_heads(2, nc.gpsimd)
         residual_gpsimd(3)
         residual_out(2, 0)
-        residual_tensor(2, D, TENSOR_COLS)
+        residual_tensor(2, D, TENSOR_COLS, "qc")
         quantise(3, 0, GC)
         first_matmul(3)
         means(1)
@@ -500,8 +538,9 @@ def tile_crossmodalattention_pa_t_kernel(
         centre(1)
         add_value_bias(3)
         residual_out(3, 0)
-        residual_tensor(3, D, TENSOR_COLS)
+        residual_tensor(3, D, TENSOR_COLS, "qc")
         residual_out(3, D)
+        transpose_kv(5)
 
         def at(lag, fn, *args):
             if tick - lag < NG:
@@ -511,25 +550,22 @@ def tile_crossmodalattention_pa_t_kernel(
             if tick % 4 == 0:
                 load_chunk(kv_view, kv_tiles, "kv", tick // 4 + 3)
                 load_chunk(q_view, q_tiles, "q", tick // 4 + 3)
+            if tick > 4: at(3, means)
+            if tick + 1 < NG: copy_kv(tick + 1, scopy)
+            if tick > 4: at(3, square, 0)
             if tick - 1 < NG: release_gpsimd(tick - 1); weigh_heads(tick - 1, nc.gpsimd)
             if tick < NG: residual_gpsimd(tick)
             if tick < NG + 2: quantise(tick, 0 if tick < NG else GC, 2 * GC)
             at(0, first_matmul)
-            if tick + 1 < NG: transpose_kv(tick + 1)
             at(2, second_matmul)
+            if tick + 2 < NG: transpose_kv(tick + 2)
             at(0, residual_tensor, 0, D)
+            at(0, residual_tensor, D, TENSOR_COLS, "qc")
             if tick > 4 and tick - 4 < NG: finish(tick - 4, 0); finish(tick - 4, 1); store(tick - 4)
             if tick > 4: at(3, centre)
             at(0, add_value_bias)
-            if tick > 4: at(3, deviation)
-            if tick + 1 < NG: copy_kv(tick + 1, scopy)
-            if tick % 2 == 0 and 2 * tick + 8 < NT: widen_head_weights(2 * tick + 8, 2 * tick + 12, scopy)
-            at(0, residual_tensor, D, TENSOR_COLS, "kvT")
+            if tick > 4: at(3, square, 1)
             at(0, residual_out, 0)
-            if tick % 2 == 1 and 3 < tick and 2 * tick + 6 < NT: transpose_head_weights(2 * tick + 6, 2 * tick + 10, "qb")
-            at(2, add_residual)
-            at(2, means)
+            if tick > 4: at(3, deviation)
             at(0, residual_out, D)
-            if tick % 2 == 1 and 3 < tick and 2 * tick + 6 < NT: copy_head_weights(2 * tick + 6, 2 * tick + 10, scopy)
-            at(2, square, 0)
-            at(2, square, 1)
+            at(2, add_residual)

@@ -60,9 +60,14 @@ def tile_crossmodalattention_pa_t_kernel(
             for j in range(j0, j1):
                 store[j] = (t, (j - j0) * D)
 
-        load_chunk(kv_view, kv_tiles, "kv", 0)
-        w_sb = const.tile([P, 4 * D], BF16, name="w_sb")
-        nc.sync.dma_start(out=w_sb[:], in_=w_v.rearrange("(p t) k -> p (t k)", t=4))
+        w_view = w_v.rearrange("(p t) k -> p (t k)", t=4)
+        w_halves = []
+        for i in range(2):
+            half = const.tile([P, 2 * D], BF16, name="w_sb%d" % i)
+            nc.sync.dma_start(out=half[:], in_=w_view[:, 2 * i * D : 2 * (i + 1) * D])
+            w_halves.append(half)
+            if i == 0:
+                load_chunk(kv_view, kv_tiles, "kv", 0)
         aw_sb = const.tile([P, NT * 8], BF16, name="aw_sb")
         nc.sync.dma_start(out=aw_sb[:], in_=attn_w.rearrange("(p j) h o -> p (j h o)", j=NT))
         rows = const.tile([P, 3 * D], BF16, name="rows")
@@ -79,7 +84,7 @@ def tile_crossmodalattention_pa_t_kernel(
             in_=out_w.rearrange("(nb p) d -> p nb d", p=P),
         )
         load_chunk(q_view, q_tiles, "q", 0)
-        for i in range(1, 4):
+        for i in range(1, 5):
             load_chunk(kv_view, kv_tiles, "kv", i)
             load_chunk(q_view, q_tiles, "q", i)
 
@@ -115,11 +120,15 @@ def tile_crossmodalattention_pa_t_kernel(
                 in_=bank[:].rearrange("w (s h c) -> w s c h", s=2, h=2),
             )
 
-        def quantise_weight(grouped, prefix):
+        def weight_codes(prefix):
             codes = const.tile([P, D], U32, name=prefix + "c", align_bytes=64)
             scales = const.tile([P, D], U8, name=prefix + "s", align_bytes=64)
-            nc.vector.quantize_mx(out=codes[:].bitcast(FP8X4), scales=scales[:], in_=grouped[:])
             return codes, scales
+
+        def quantise_weight(grouped, codes, scales, lo, hi):
+            nc.vector.quantize_mx(
+                out=codes[:, lo:hi].bitcast(FP8X4), scales=scales[:, lo:hi], in_=grouped[:, 4 * lo : 4 * hi]
+            )
 
         def spread(i, tag, name):
             bank = psum.tile([P, D], F32, name=name, tag=tag)
@@ -150,7 +159,7 @@ def tile_crossmodalattention_pa_t_kernel(
             flat = out.rearrange("r n -> (r n)")
             size = P * 16 * P
             base = B * D - nblk * size
-            awT = psum.tile([P, nblk * P], BF16, name="awT2", tag="kvT")
+            awT = psum.tile([P, nblk * P], BF16, name="awT2", tag="qc")
             for i in range(nblk):
                 lo = (ENGINE_TILES + 16 * i) * 8
                 nc.tensor.transpose(awT[:, i * P : (i + 1) * P], aw_sb[:, lo : lo + P], ident_b[:])
@@ -405,26 +414,26 @@ def tile_crossmodalattention_pa_t_kernel(
                 )
             st["o", c] = o
 
-        def finish(c, jj):
+        def finish(c):
             rstd = st["rstd", c]
             o = st["o", c]
-            nc.vector.scalar_tensor_tensor(
-                out=o[:, jj * D : (jj + 1) * D],
-                in0=o[:, jj * D : (jj + 1) * D],
-                scalar=rstd[:, jj : jj + 1],
-                in1=gb_ps[:, D : 2 * D],
-                op0=ALU.mult,
-                op1=ALU.add,
-            )
-
-        def store(c, lo=0, hi=GW):
-            nc.sync.dma_start(
-                out=out_view[:, c * GW + lo : c * GW + hi], in_=st["o", c][:, lo:hi]
-            )
+            for jj in range(GT):
+                lo, hi = jj * D, (jj + 1) * D
+                nc.vector.scalar_tensor_tensor(
+                    out=o[:, lo:hi],
+                    in0=o[:, lo:hi],
+                    scalar=rstd[:, jj : jj + 1],
+                    in1=gb_ps[:, D : 2 * D],
+                    op0=ALU.mult,
+                    op1=ALU.add,
+                )
+                if c == NG - 1:
+                    nc.sync.dma_start(out=out_view[:, c * GW + lo : c * GW + hi], in_=o[:, lo:hi])
+            if c < NG - 1:
+                nc.sync.dma_start(out=out_view[:, c * GW : (c + 1) * GW], in_=o[:])
 
         vcopy = nc.vector.tensor_copy
         scopy = nc.scalar.copy
-        w_f = w_sb[:].bitcast(F32)
         ow_f = ow_sb[:].bitcast(F32).rearrange("n (nb q a) -> n nb a q", nb=4, a=2)
         bv = const.tile([P, 4], F32, name="bv")
         wg = const.tile([P, 4 * D], BF16, name="wg", align_bytes=64)
@@ -432,72 +441,66 @@ def tile_crossmodalattention_pa_t_kernel(
         ob_cols = const.tile([P, D], F32, name="ob_cols")
         ob_sb = const.tile([P, D], BF16, name="ob_sb")
 
-        transpose_kv(0)
-        copy_kv(0, scopy)
+        wc, ws = weight_codes("w")
+        oc, os_ = weight_codes("o")
+
         def w_words(t, u):
-            return w_f[:, t * 256 + u : (t + 1) * 256 : 2]
+            t_f = w_halves[t // 2][:].bitcast(F32)
+            return t_f[:, (t % 2) * 256 + u : (t % 2 + 1) * 256 : 2]
 
         def ow_words(nb, a):
             return ow_f[:, nb, a, :]
 
         w_a = transpose_weight(w_words, 0, "s1a", "w")
+        weight_out(w_a, 0, wg, scopy)
+        transpose_kv(0)
+        copy_kv(0, scopy)
         w_b = transpose_weight(w_words, 1, "s1b", "w")
         widen_head_weights(0, 8, vcopy)
+        quantise_weight(wg, wc, ws, 0, GC)
         quantise(0, 0, GC)
-        widen_head_weights(8, 16, vcopy)
-        weight_out(w_a, 0, wg, scopy)
         weight_out(w_b, 1, wg, vcopy)
-        transpose_head_weights(0, 8, "qb")
-        transpose_head_weights(8, 16, "kvT")
+        widen_head_weights(8, 16, vcopy)
+        quantise_weight(wg, wc, ws, GC, 2 * GC)
         obT = psum.tile([P, D], BF16, name="obT", tag="qc")
         for n in range(4):
             nc.tensor.transpose(
                 obT[:, n * P : (n + 1) * P], rows[:, 2 * D + n * P : 2 * D + (n + 1) * P], ident_b[:]
             )
         ob_ps = spread(2, "gb", "ob_ps")
+        transpose_head_weights(0, 8, "qb")
         nc.scalar.copy(
             out=ob_cols[:].rearrange("p (n m) -> p n m", n=4),
             in_=obT[:].rearrange("p (n m) -> p n m", n=4)[:, :, 0:1].to_broadcast([P, 4, P]),
         )
         nc.scalar.copy(out=ob_sb[:], in_=ob_ps[:])
-        wc, ws = quantise_weight(wg, "w")
-        nc.vector.tensor_copy(out=bv[:], in_=bv_bf[:])
+        nc.scalar.copy(out=bv[:], in_=bv_bf[:])
         copy_head_weights(0, 8, vcopy)
-        copy_head_weights(8, 16, vcopy)
-        spread_head_weights()
         first_matmul(0)
         o_a = transpose_weight(ow_words, 0, "s2a", "o")
         o_b = transpose_weight(ow_words, 1, "s2b", "o")
         transpose_kv(1)
         residual_tensor(0, 0, D)
+        residual_tensor(0, D, TENSOR_COLS, "qc")
         weight_out(o_a, 0, og, scopy)
-        weight_out(o_b, 1, og, scopy)
-        copy_kv(1, scopy)
+        weigh_heads_vector(0)
+        weight_out(o_b, 1, og, vcopy)
+        interleave(0, scopy)
+        copy_kv(1, vcopy)
         transpose_kv(2)
         residual_out(0, 0)
-        residual_tensor(0, D, TENSOR_COLS, "qc")
+        residual_out(0, D)
+        copy_kv(2, scopy)
         residual_gpsimd(0)
         residual_gpsimd(1)
-        weigh_heads_vector(0)
-        oc, os_ = quantise_weight(og, "o")
-        interleave(0, scopy)
-        quantise(1, 0, GC)
-        first_matmul(1)
-        residual_out(0, D)
-        quantise(2, GC, 2 * GC)
-        second_matmul(0)
-        residual_tensor(1, 0, D)
-        weigh_heads_vector(1)
-        copy_kv(2, scopy)
-        transpose_kv(3)
-        residual_out(1, 0)
-        residual_tensor(1, D, TENSOR_COLS, "qc")
-        add_residual(0)
-        interleave(1, scopy)
-        residual_out(1, D)
-        quantise(2, 0, GC)
-        first_matmul(2)
         residual_gpsimd(2)
+        residual_tensor(1, 0, D)
+        residual_tensor(1, D, TENSOR_COLS, "qc")
+        quantise_weight(og, oc, os_, 0, 2 * GC)
+        quantise(1, 0, GC)
+        quantise(2, GC, 2 * GC)
+        first_matmul(1)
+        second_matmul(0)
         gb_ps = psum.tile([P, 2 * D], BF16, name="gb_ps", tag="gb")
         for i in range(2):
             nc.tensor.matmul(
@@ -507,40 +510,42 @@ def tile_crossmodalattention_pa_t_kernel(
                 start=True,
                 stop=True,
             )
+        transpose_kv(3)
+        residual_out(1, 0)
+        residual_out(1, D)
+        transpose_head_weights(8, 16, "qb")
+        copy_kv(3, scopy)
+        quantise(2, 0, GC)
+        weigh_heads_vector(1)
+        first_matmul(2)
+        interleave(1, scopy)
+        add_residual(0)
         means(0)
-        quantise(3, GC, 2 * GC)
+        copy_head_weights(8, 16, vcopy)
+        spread_head_weights()
+        quantise(3, 0, 2 * GC)
         second_matmul(1)
         add_value_bias(2)
+        residual_gpsimd(3)
+        weigh_heads(2, nc.gpsimd)
+        residual_tensor(2, 0, D)
+        residual_tensor(2, D, TENSOR_COLS, "qc")
         square(0, 0)
         square(0, 1)
-        residual_tensor(2, 0, D)
-        copy_kv(3, scopy)
-        transpose_kv(4)
         deviation(0)
+        first_matmul(3)
+        transpose_kv(4)
+        residual_out(2, 0)
+        residual_out(2, D)
         centre(0)
         add_residual(1)
-        weigh_heads(2, nc.gpsimd)
-        residual_gpsimd(3)
-        residual_out(2, 0)
-        residual_tensor(2, D, TENSOR_COLS, "qc")
-        quantise(3, 0, GC)
-        first_matmul(3)
-        means(1)
-        square(1, 0)
-        square(1, 1)
-        residual_out(2, D)
-        residual_tensor(3, 0, D)
-        deviation(1)
         copy_kv(4, scopy)
-        finish(0, 0)
-        finish(0, 1)
-        store(0)
-        centre(1)
         add_value_bias(3)
-        residual_out(3, 0)
-        residual_tensor(3, D, TENSOR_COLS, "qc")
-        residual_out(3, D)
         transpose_kv(5)
+        residual_tensor(3, 0, D)
+        residual_tensor(3, D, TENSOR_COLS, "qc")
+        residual_out(3, 0)
+        residual_out(3, D)
 
         def at(lag, fn, *args):
             if tick - lag < NG:
@@ -548,24 +553,25 @@ def tile_crossmodalattention_pa_t_kernel(
 
         for tick in range(4, NG + 6):
             if tick % 4 == 0:
-                load_chunk(kv_view, kv_tiles, "kv", tick // 4 + 3)
-                load_chunk(q_view, q_tiles, "q", tick // 4 + 3)
-            if tick > 4: at(3, means)
+                load_chunk(kv_view, kv_tiles, "kv", tick // 4 + 4)
+                load_chunk(q_view, q_tiles, "q", tick // 4 + 4)
+            at(3, means)
             if tick + 1 < NG: copy_kv(tick + 1, scopy)
-            if tick > 4: at(3, square, 0)
-            if tick - 1 < NG: release_gpsimd(tick - 1); weigh_heads(tick - 1, nc.gpsimd)
+            at(3, square, 0)
             if tick < NG: residual_gpsimd(tick)
+            if tick == NG: release_gpsimd(tick - 1)
+            if tick - 1 < NG: weigh_heads(tick - 1, nc.gpsimd)
             if tick < NG + 2: quantise(tick, 0 if tick < NG else GC, 2 * GC)
             at(0, first_matmul)
             at(2, second_matmul)
             if tick + 2 < NG: transpose_kv(tick + 2)
             at(0, residual_tensor, 0, D)
             at(0, residual_tensor, D, TENSOR_COLS, "qc")
-            if tick > 4 and tick - 4 < NG: finish(tick - 4, 0); finish(tick - 4, 1); store(tick - 4)
-            if tick > 4: at(3, centre)
+            if tick - 4 < NG: finish(tick - 4)
+            at(3, centre)
             at(0, add_value_bias)
-            if tick > 4: at(3, square, 1)
+            at(3, square, 1)
             at(0, residual_out, 0)
-            if tick > 4: at(3, deviation)
+            at(3, deviation)
             at(0, residual_out, D)
             at(2, add_residual)

@@ -208,18 +208,19 @@ def tile_crossmodalattention_pa_t_kernel(
                 )
             st["qb", c, lo] = (bank, hi)
 
-        def residual_out(c, lo, copy=nc.scalar.copy):
-            bank, hi = st["qb", c, lo]
+        def residual_tile(c):
             if ("qp", c) not in st:
                 st["qp", c] = w3.tile([P, GW], F32, name="qp", tag="qp")
-            copy(out=st["qp", c][:, lo:hi], in_=bank[:, 0 : hi - lo])
+            return st["qp", c]
+
+        def residual_out(c, lo):
+            bank, hi = st["qb", c, lo]
+            nc.scalar.copy(out=residual_tile(c)[:, lo:hi], in_=bank[:, 0 : hi - lo])
 
         def residual_gpsimd(c):
             t, off = q_tiles[GT * c]
-            if ("qp", c) not in st:
-                st["qp", c] = w3.tile([P, GW], F32, name="qp", tag="qp")
             nc.gpsimd.tensor_tensor(
-                out=st["qp", c][:, TENSOR_COLS:GW],
+                out=residual_tile(c)[:, TENSOR_COLS:GW],
                 in0=t[:, off + TENSOR_COLS : off + GW],
                 in1=ob_sb[:, TENSOR_COLS - D : D],
                 op=ALU.add,
@@ -414,6 +415,17 @@ def tile_crossmodalattention_pa_t_kernel(
                 )
             st["o", c] = o
 
+        def finish_shared(c):
+            rstd = st["rstd", c]
+            o = st["o", c]
+            for jj in range(GT):
+                lo, hi = jj * D, (jj + 1) * D
+                nc.scalar.activation(
+                    out=o[:, lo:hi], in_=o[:, lo:hi], func=ACT.Copy, scale=rstd[:, jj : jj + 1]
+                )
+                nc.gpsimd.tensor_tensor(out=o[:, lo:hi], in0=o[:, lo:hi], in1=b_sb[:], op=ALU.add)
+            nc.sync.dma_start(out=out_view[:, c * GW : (c + 1) * GW], in_=o[:])
+
         def finish(c):
             rstd = st["rstd", c]
             o = st["o", c]
@@ -440,6 +452,7 @@ def tile_crossmodalattention_pa_t_kernel(
         og = const.tile([P, 4 * D], BF16, name="og", align_bytes=64)
         ob_cols = const.tile([P, D], F32, name="ob_cols")
         ob_sb = const.tile([P, D], BF16, name="ob_sb")
+        b_sb = const.tile([P, D], BF16, name="b_sb")
 
         wc, ws = weight_codes("w")
         oc, os_ = weight_codes("o")
@@ -493,14 +506,13 @@ def tile_crossmodalattention_pa_t_kernel(
         copy_kv(2, scopy)
         residual_gpsimd(0)
         residual_gpsimd(1)
-        residual_gpsimd(2)
+        quantise(1, 0, GC)
+        first_matmul(1)
+        quantise_weight(og, oc, os_, 0, 2 * GC)
+        quantise(2, GC, 2 * GC)
+        second_matmul(0)
         residual_tensor(1, 0, D)
         residual_tensor(1, D, TENSOR_COLS, "qc")
-        quantise_weight(og, oc, os_, 0, 2 * GC)
-        quantise(1, 0, GC)
-        quantise(2, GC, 2 * GC)
-        first_matmul(1)
-        second_matmul(0)
         gb_ps = psum.tile([P, 2 * D], BF16, name="gb_ps", tag="gb")
         for i in range(2):
             nc.tensor.matmul(
@@ -514,11 +526,11 @@ def tile_crossmodalattention_pa_t_kernel(
         residual_out(1, 0)
         residual_out(1, D)
         transpose_head_weights(8, 16, "qb")
+        weigh_heads_vector(1)
+        interleave(1, scopy)
         copy_kv(3, scopy)
         quantise(2, 0, GC)
-        weigh_heads_vector(1)
         first_matmul(2)
-        interleave(1, scopy)
         add_residual(0)
         means(0)
         copy_head_weights(8, 16, vcopy)
@@ -526,26 +538,30 @@ def tile_crossmodalattention_pa_t_kernel(
         quantise(3, 0, 2 * GC)
         second_matmul(1)
         add_value_bias(2)
+        residual_tile(2)
         residual_gpsimd(3)
+        residual_gpsimd(2)
         weigh_heads(2, nc.gpsimd)
         residual_tensor(2, 0, D)
         residual_tensor(2, D, TENSOR_COLS, "qc")
         square(0, 0)
         square(0, 1)
         deviation(0)
-        first_matmul(3)
         transpose_kv(4)
+        first_matmul(3)
+        copy_kv(4, scopy)
         residual_out(2, 0)
         residual_out(2, D)
         centre(0)
         add_residual(1)
-        copy_kv(4, scopy)
         add_value_bias(3)
         transpose_kv(5)
         residual_tensor(3, 0, D)
         residual_tensor(3, D, TENSOR_COLS, "qc")
         residual_out(3, 0)
         residual_out(3, D)
+
+        SHARED = (NG - 2,)
 
         def at(lag, fn, *args):
             if tick - lag < NG:
@@ -567,11 +583,13 @@ def tile_crossmodalattention_pa_t_kernel(
             if tick + 2 < NG: transpose_kv(tick + 2)
             at(0, residual_tensor, 0, D)
             at(0, residual_tensor, D, TENSOR_COLS, "qc")
-            if tick - 4 < NG: finish(tick - 4)
+            if tick - 4 < NG and tick - 4 not in SHARED: finish(tick - 4)
             at(3, centre)
             at(0, add_value_bias)
             at(3, square, 1)
             at(0, residual_out, 0)
             at(3, deviation)
             at(0, residual_out, D)
+            if tick == NG: nc.scalar.copy(out=b_sb[:], in_=gb_ps[:, D : 2 * D])
+            if tick - 3 in SHARED: finish_shared(tick - 3)
             at(2, add_residual)

@@ -574,21 +574,21 @@ def tile_crossmodalattention_pa_t_kernel(
             at(3, means)
             if tick + 1 < NG: copy_kv(tick + 1, scopy)
             at(3, square, 0)
+            at(3, square, 1)
             if tick < NG: residual_gpsimd(tick)
             if tick == NG: release_gpsimd(tick - 1)
             if tick - 1 < NG: weigh_heads(tick - 1, nc.gpsimd)
             if tick < NG + 2: quantise(tick, 0 if tick < NG else GC, 2 * GC)
-            at(0, first_matmul)
             at(2, second_matmul)
+            at(0, first_matmul)
             if tick + 2 < NG: transpose_kv(tick + 2)
             at(0, residual_tensor, 0, D)
             at(0, residual_tensor, D, TENSOR_COLS, "qc")
             if tick - 4 < NG and tick - 4 not in SHARED: finish(tick - 4)
             at(3, centre)
             at(0, add_value_bias)
-            at(3, square, 1)
-            at(0, residual_out, 0)
             at(3, deviation)
+            at(0, residual_out, 0)
             at(0, residual_out, D)
             if tick == NG: nc.scalar.copy(out=b_sb[:], in_=gb_ps[:, D : 2 * D])
             if tick - 3 in SHARED: finish_shared(tick - 3)

@@ -78,12 +78,12 @@ def tile_crossmodalattention_pa_t_kernel(
             nc.sync.dma_start(
                 out=rows[0:1, i * D : (i + 1) * D], in_=vec.rearrange("(o n) -> o n", o=1)
             )
+        load_chunk(q_view, q_tiles, "q", 0)
         ow_sb = const.tile([P, 4 * D], BF16, name="ow_sb")
         nc.sync.dma_start(
             out=ow_sb[:].rearrange("p (nb d) -> p nb d", nb=4),
             in_=out_w.rearrange("(nb p) d -> p nb d", p=P),
         )
-        load_chunk(q_view, q_tiles, "q", 0)
         for i in range(1, 5):
             load_chunk(kv_view, kv_tiles, "kv", i)
             load_chunk(q_view, q_tiles, "q", i)
@@ -137,21 +137,29 @@ def tile_crossmodalattention_pa_t_kernel(
             )
             return bank
 
+        awx = const.tile([P, ENGINE_TILES * P], BF16, name="awx")
+
         def widen_head_weights(j0, j1, copy):
-            awx = w2.tile([P, BLK * P], BF16, name="awx", tag="awx")
             copy(
-                out=awx[:, 0 : (j1 - j0) * P].rearrange("p (m r) -> p m r", r=16),
+                out=awx[:, j0 * P : j1 * P].rearrange("p (m r) -> p m r", r=16),
                 in_=aw_sb[:, j0 * 8 : j1 * 8].unsqueeze(2).to_broadcast([P, (j1 - j0) * 8, 16]),
             )
-            st["awx", j0] = awx
+
+        def widen_gpsimd(j0, j1):
+            nc.gpsimd.tensor_scalar(
+                out=awx[:, j0 * P : j1 * P].rearrange("p (m r) -> p m r", r=16),
+                in0=aw_sb[:, j0 * 8 : j1 * 8].unsqueeze(2).to_broadcast([P, (j1 - j0) * 8, 16]),
+                scalar1=1.0,
+                scalar2=0.0,
+                op0=ALU.mult,
+                op1=ALU.add,
+            )
 
         def transpose_head_weights(j0, j1, tag="kvT"):
-            awx = st["awx", j0]
             awT = psum.tile([P, BLK * P], BF16, name="awT", tag=tag)
             for j in range(j1 - j0):
-                nc.tensor.transpose(
-                    awT[:, j * P : (j + 1) * P], awx[:, j * P : (j + 1) * P], ident_b[:]
-                )
+                lo = (j0 + j) * P
+                nc.tensor.transpose(awT[:, j * P : (j + 1) * P], awx[:, lo : lo + P], ident_b[:])
             st["awT", j0] = awT
 
         def spread_head_weights():
@@ -159,12 +167,12 @@ def tile_crossmodalattention_pa_t_kernel(
             flat = out.rearrange("r n -> (r n)")
             size = P * 16 * P
             base = B * D - nblk * size
-            awT = psum.tile([P, nblk * P], BF16, name="awT2", tag="qc")
+            awT = psum.tile([P, nblk * P], BF16, name="awT2", tag="s2a")
             for i in range(nblk):
                 lo = (ENGINE_TILES + 16 * i) * 8
                 nc.tensor.transpose(awT[:, i * P : (i + 1) * P], aw_sb[:, lo : lo + P], ident_b[:])
             awS = const.tile([P, nblk * P], F32, name="awS")
-            nc.vector.tensor_copy(out=awS[:], in_=awT[:])
+            nc.scalar.copy(out=awS[:], in_=awT[:])
             segs = [flat[base + i * size : base + (i + 1) * size] for i in range(nblk)]
             for i in range(nblk):
                 nc.sync.dma_start(
@@ -200,7 +208,7 @@ def tile_crossmodalattention_pa_t_kernel(
             for n in range(0, hi - lo, P):
                 nc.tensor.matmul(
                     out=bank[:, n : n + P],
-                    lhsT=ob_cols[:, n : n + P],
+                    lhsT=ob_cols[:, lo % D + n : lo % D + n + P],
                     rhs=ident_f[:],
                     is_transpose=True,
                     start=False,
@@ -246,8 +254,8 @@ def tile_crossmodalattention_pa_t_kernel(
                 in_=qin(k)[:, 4 * lo : 4 * hi],
             )
 
-        def transpose_kv(c):
-            kvT = psum.tile([P, D], F32, name="kvT", tag="kvT")
+        def transpose_kv(c, tag="kvT"):
+            kvT = psum.tile([P, D], F32, name="kvT", tag=tag)
             for jj in range(GT):
                 t, off = kv_tiles[GT * c + jj]
                 t_f = t[:].bitcast(F32)
@@ -299,24 +307,27 @@ def tile_crossmodalattention_pa_t_kernel(
                 )
             st["planes", c] = planes
 
-        def weigh_heads_vector(c):
+        def weigh_heads_vector(c, lo, hi):
             banks = st["s1", c]
-            planes = w2.tile([P, 4 * GC], BF16, name="planes_v", tag="planes")
+            if lo == 0:
+                st["planes_v", c] = w2.tile([P, 4 * GC], BF16, name="planes_v", tag="planes")
+            planes = st["planes_v", c]
             for t in range(4):
                 nc.vector.scalar_tensor_tensor(
-                    out=planes[:, t * GC : (t + 1) * GC],
-                    in0=banks[t // 2][:, (t % 2) * GC : (t % 2 + 1) * GC],
+                    out=planes[:, t * GC + lo : t * GC + hi],
+                    in0=banks[t // 2][:, (t % 2) * GC + lo : (t % 2) * GC + hi],
                     scalar=bv[:, t : t + 1],
-                    in1=head_weights(c),
+                    in1=head_weights(c)[:, lo:hi],
                     op0=ALU.add,
                     op1=ALU.mult,
                 )
-            st["planes_v", c] = planes
 
-        def interleave(c, copy):
+        def interleave(c, lo, hi, copy):
             copy(
-                out=attn_half(c).rearrange("p (c i t) -> p c t i", i=4, t=4),
-                in_=st["planes_v", c][:].rearrange("p (t c i) -> p c t i", t=4, i=4),
+                out=attn_half(c)[:, 4 * lo : 4 * hi].rearrange("p (c i t) -> p c t i", i=4, t=4),
+                in_=st["planes_v", c][:]
+                .rearrange("p (t w) -> p t w", t=4)[:, :, lo:hi]
+                .rearrange("p t (c i) -> p c t i", i=4),
             )
 
         def weigh_heads(c, engine):
@@ -331,8 +342,7 @@ def tile_crossmodalattention_pa_t_kernel(
             )
 
         def release_gpsimd(c):
-            first = 0 if c + 1 < NG else 4 * GC
-            nc.vector.tensor_copy(out=attn_half(c)[:, 0:1], in_=qin(c + 1)[:, first : first + 1])
+            nc.vector.tensor_copy(out=attn_half(c)[:, 0:1], in_=attn_half(c - 1)[:, 0:1])
 
         def second_matmul(c):
             codes, scales = st["codes", c + 2]
@@ -352,11 +362,23 @@ def tile_crossmodalattention_pa_t_kernel(
                 )
             st["s2", c] = banks
 
-        def add_residual(c):
+        def residual_vector(c, jj):
+            t, off = q_tiles[GT * c + jj]
+            nc.vector.tensor_tensor(
+                out=residual_tile(c)[:, jj * D : (jj + 1) * D],
+                in0=t[:, off : off + D],
+                in1=ob_sb[:],
+                op=ALU.add,
+            )
+
+        def add_residual(c, tiles=range(GT)):
             banks = st["s2", c]
-            z = w2.tile([P, GW], F32, name="z", tag="z")
-            sums = w3.tile([P, GT], F32, name="sums", tag="sums")
-            for jj in range(GT):
+            if ("z", c) not in st:
+                z = w2.tile([P, GW], F32, name="z", tag="z")
+                sums = w3.tile([P, GT], F32, name="sums", tag="sums")
+                st["z", c] = (z, sums)
+            z, sums = st["z", c]
+            for jj in tiles:
                 nc.vector.scalar_tensor_tensor(
                     out=z[:, jj * D : (jj + 1) * D],
                     in0=banks[jj][:],
@@ -366,7 +388,6 @@ def tile_crossmodalattention_pa_t_kernel(
                     op1=ALU.add,
                     accum_out=sums[:, jj : jj + 1],
                 )
-            st["z", c] = (z, sums)
 
         def means(c):
             z, sums = st["z", c]
@@ -424,7 +445,7 @@ def tile_crossmodalattention_pa_t_kernel(
                     out=o[:, lo:hi], in_=o[:, lo:hi], func=ACT.Copy, scale=rstd[:, jj : jj + 1]
                 )
                 nc.gpsimd.tensor_tensor(out=o[:, lo:hi], in0=o[:, lo:hi], in1=b_sb[:], op=ALU.add)
-            nc.sync.dma_start(out=out_view[:, c * GW : (c + 1) * GW], in_=o[:])
+                nc.sync.dma_start(out=out_view[:, c * GW + lo : c * GW + hi], in_=o[:, lo:hi])
 
         def finish(c):
             rstd = st["rstd", c]
@@ -466,53 +487,31 @@ def tile_crossmodalattention_pa_t_kernel(
 
         w_a = transpose_weight(w_words, 0, "s1a", "w")
         weight_out(w_a, 0, wg, scopy)
+        widen_gpsimd(0, 4)
         transpose_kv(0)
-        copy_kv(0, scopy)
+        copy_kv(0, vcopy)
         w_b = transpose_weight(w_words, 1, "s1b", "w")
-        widen_head_weights(0, 8, vcopy)
         quantise_weight(wg, wc, ws, 0, GC)
+        weight_out(w_b, 1, wg, scopy)
+        transpose_head_weights(0, 4, "qb")
         quantise(0, 0, GC)
-        weight_out(w_b, 1, wg, vcopy)
-        widen_head_weights(8, 16, vcopy)
         quantise_weight(wg, wc, ws, GC, 2 * GC)
+        copy_head_weights(0, 4, scopy)
+        nc.scalar.copy(out=bv[:], in_=bv_bf[:])
+        ob_ps = spread(2, "gb", "ob_ps")
+        first_matmul(0)
+        nc.scalar.copy(out=ob_sb[:], in_=ob_ps[:])
         obT = psum.tile([P, D], BF16, name="obT", tag="qc")
         for n in range(4):
             nc.tensor.transpose(
                 obT[:, n * P : (n + 1) * P], rows[:, 2 * D + n * P : 2 * D + (n + 1) * P], ident_b[:]
             )
-        ob_ps = spread(2, "gb", "ob_ps")
-        transpose_head_weights(0, 8, "qb")
+        widen_head_weights(4, 12, scopy)
         nc.scalar.copy(
             out=ob_cols[:].rearrange("p (n m) -> p n m", n=4),
             in_=obT[:].rearrange("p (n m) -> p n m", n=4)[:, :, 0:1].to_broadcast([P, 4, P]),
         )
-        nc.scalar.copy(out=ob_sb[:], in_=ob_ps[:])
-        nc.scalar.copy(out=bv[:], in_=bv_bf[:])
-        copy_head_weights(0, 8, vcopy)
-        first_matmul(0)
-        o_a = transpose_weight(ow_words, 0, "s2a", "o")
-        o_b = transpose_weight(ow_words, 1, "s2b", "o")
-        transpose_kv(1)
-        residual_tensor(0, 0, D)
-        residual_tensor(0, D, TENSOR_COLS, "qc")
-        weight_out(o_a, 0, og, scopy)
-        weigh_heads_vector(0)
-        weight_out(o_b, 1, og, vcopy)
-        interleave(0, scopy)
-        copy_kv(1, vcopy)
-        transpose_kv(2)
-        residual_out(0, 0)
-        residual_out(0, D)
-        copy_kv(2, scopy)
-        residual_gpsimd(0)
-        residual_gpsimd(1)
-        quantise(1, 0, GC)
-        first_matmul(1)
-        quantise_weight(og, oc, os_, 0, 2 * GC)
-        quantise(2, GC, 2 * GC)
-        second_matmul(0)
-        residual_tensor(1, 0, D)
-        residual_tensor(1, D, TENSOR_COLS, "qc")
+        spread_head_weights()
         gb_ps = psum.tile([P, 2 * D], BF16, name="gb_ps", tag="gb")
         for i in range(2):
             nc.tensor.matmul(
@@ -522,74 +521,107 @@ def tile_crossmodalattention_pa_t_kernel(
                 start=True,
                 stop=True,
             )
-        transpose_kv(3)
-        residual_out(1, 0)
-        residual_out(1, D)
-        transpose_head_weights(8, 16, "qb")
-        weigh_heads_vector(1)
-        interleave(1, scopy)
-        copy_kv(3, scopy)
+        residual_vector(0, 0)
+        transpose_kv(1, "qb")
+        copy_kv(1, scopy)
+        o_a = transpose_weight(ow_words, 0, "s2a", "o")
+        o_b = transpose_weight(ow_words, 1, "s2b", "o")
+        transpose_kv(2)
+        residual_gpsimd(1)
+        weigh_heads_vector(0, 0, P)
+        weigh_heads_vector(0, P, GC)
+        interleave(0, 0, P, scopy)
+        interleave(0, P, GC, scopy)
+        weight_out(o_a, 0, og, vcopy)
+        quantise(1, 0, GC)
+        first_matmul(1)
+        weight_out(o_b, 1, og, vcopy)
+        copy_kv(2, scopy)
+        quantise(2, GC, 2 * GC)
+        quantise_weight(og, oc, os_, 0, 2 * GC)
+        transpose_head_weights(4, 12, "qb")
+        second_matmul(0)
         quantise(2, 0, GC)
+        residual_vector(0, 1)
+        add_value_bias(1)
+        copy_head_weights(4, 12, scopy)
+        widen_head_weights(12, 16, scopy)
+        nc.scalar.copy(out=b_sb[:], in_=gb_ps[:, D : 2 * D])
         first_matmul(2)
-        add_residual(0)
-        means(0)
-        copy_head_weights(8, 16, vcopy)
-        spread_head_weights()
-        quantise(3, 0, 2 * GC)
-        second_matmul(1)
         add_value_bias(2)
-        residual_tile(2)
-        residual_gpsimd(3)
+        transpose_kv(3, "qc")
+        weigh_heads(1, nc.gpsimd)
+        transpose_head_weights(12, 16, "kvT")
+        add_residual(0)
+        copy_kv(3, vcopy)
+        means(0)
+        copy_head_weights(12, 16, scopy)
+        residual_tensor(1, 0, D)
+        residual_tensor(1, D, TENSOR_COLS, "qc")
+        transpose_kv(4)
         residual_gpsimd(2)
-        weigh_heads(2, nc.gpsimd)
-        residual_tensor(2, 0, D)
-        residual_tensor(2, D, TENSOR_COLS, "qc")
         square(0, 0)
         square(0, 1)
         deviation(0)
-        transpose_kv(4)
-        first_matmul(3)
-        copy_kv(4, scopy)
-        residual_out(2, 0)
-        residual_out(2, D)
+        residual_out(1, 0)
+        residual_out(1, D)
         centre(0)
+        release_gpsimd(2)
+        quantise(3, 0, 2 * GC)
+        weigh_heads(2, nc.gpsimd)
+        second_matmul(1)
+        first_matmul(3)
+        copy_kv(4, vcopy)
+        finish(0)
         add_residual(1)
         add_value_bias(3)
+        residual_tensor(2, 0, D)
+        residual_tensor(2, D, TENSOR_COLS, "qc")
+        residual_out(2, 0)
+        residual_out(2, D)
         transpose_kv(5)
-        residual_tensor(3, 0, D)
-        residual_tensor(3, D, TENSOR_COLS, "qc")
-        residual_out(3, 0)
-        residual_out(3, D)
 
-        SHARED = (NG - 2,)
+        residual_tile(3)
+
+        SHARED = (NG - 3, NG - 2)
 
         def at(lag, fn, *args):
-            if tick - lag < NG:
+            if 0 <= tick - lag < NG:
                 fn(tick - lag, *args)
 
         for tick in range(4, NG + 6):
+            if tick % 4 == 1:
+                load_chunk(q_view, q_tiles, "q", tick // 4 + 4)
             if tick % 4 == 0:
                 load_chunk(kv_view, kv_tiles, "kv", tick // 4 + 4)
-                load_chunk(q_view, q_tiles, "q", tick // 4 + 4)
-            at(3, means)
+            if tick != 5: at(3, means)
             if tick + 1 < NG: copy_kv(tick + 1, scopy)
-            at(3, square, 0)
-            at(3, square, 1)
-            if tick < NG: residual_gpsimd(tick)
-            if tick == NG: release_gpsimd(tick - 1)
+            if tick != 5: at(3, square, 0)
+            if tick != 5: at(3, square, 1)
+            if tick in (4, 5, NG): release_gpsimd(tick - 1)
+            if tick > 5 and tick < NG: residual_gpsimd(tick)
             if tick - 1 < NG: weigh_heads(tick - 1, nc.gpsimd)
-            if tick < NG + 2: quantise(tick, 0 if tick < NG else GC, 2 * GC)
+            if tick <= 5: residual_gpsimd(tick)
+            if tick <= NG: quantise(tick, 0 if tick < NG else GC, 2 * GC)
             at(2, second_matmul)
             at(0, first_matmul)
             if tick + 2 < NG: transpose_kv(tick + 2)
-            at(0, residual_tensor, 0, D)
-            at(0, residual_tensor, D, TENSOR_COLS, "qc")
-            if tick - 4 < NG and tick - 4 not in SHARED: finish(tick - 4)
+            at(1, residual_tensor, 0, D)
+            if tick == 4: residual_tensor(3, D, GW, "qc")
+            else: at(1, residual_tensor, D, TENSOR_COLS, "qc")
+            if 1 <= tick - 4 < NG and tick - 4 not in SHARED: finish(tick - 4)
             at(3, centre)
+            if tick == NG: quantise(NG + 1, GC, 2 * GC)
             at(0, add_value_bias)
-            at(3, deviation)
-            at(0, residual_out, 0)
-            at(0, residual_out, D)
-            if tick == NG: nc.scalar.copy(out=b_sb[:], in_=gb_ps[:, D : 2 * D])
+            if tick != 5: at(3, deviation)
+            if tick != 4: at(1, residual_out, 0)
+            if tick != 4: at(1, residual_out, D)
             if tick - 3 in SHARED: finish_shared(tick - 3)
             at(2, add_residual)
+            if tick == 4:
+                means(2)
+                square(2, 0)
+                square(2, 1)
+                deviation(2)
+                residual_out(3, 0)
+                residual_out(3, D)

@@ -297,7 +297,7 @@ def tile_crossmodalattention_pa_t_kernel(
         def add_value_bias(c):
             banks = st["s1", c]
             planes = w2.tile([P, 4 * GC], F32, name="planes", tag="planes")
-            for t in range(4):
+            for t in reversed(range(4)):
                 nc.scalar.activation(
                     out=planes[:, t * GC : (t + 1) * GC],
                     in_=banks[t // 2][:, (t % 2) * GC : (t % 2 + 1) * GC],
@@ -371,7 +371,7 @@ def tile_crossmodalattention_pa_t_kernel(
                 op=ALU.add,
             )
 
-        def add_residual(c, tiles=range(GT)):
+        def add_residual(c, tiles=(1, 0)):
             banks = st["s2", c]
             if ("z", c) not in st:
                 z = w2.tile([P, GW], F32, name="z", tag="z")
@@ -450,7 +450,7 @@ def tile_crossmodalattention_pa_t_kernel(
         def finish(c):
             rstd = st["rstd", c]
             o = st["o", c]
-            for jj in range(GT):
+            for jj in reversed(range(GT)):
                 lo, hi = jj * D, (jj + 1) * D
                 nc.vector.scalar_tensor_tensor(
                     out=o[:, lo:hi],
@@ -582,6 +582,7 @@ def tile_crossmodalattention_pa_t_kernel(
         transpose_kv(5)
 
         residual_tile(3)
+        residual_tile(4)
 
         SHARED = (NG - 3, NG - 2)
 
@@ -601,13 +602,13 @@ def tile_crossmodalattention_pa_t_kernel(
             if tick in (4, 5, NG): release_gpsimd(tick - 1)
             if tick > 5 and tick < NG: residual_gpsimd(tick)
             if tick - 1 < NG: weigh_heads(tick - 1, nc.gpsimd)
-            if tick <= 5: residual_gpsimd(tick)
+            if tick == 5: residual_gpsimd(tick)
             if tick <= NG: quantise(tick, 0 if tick < NG else GC, 2 * GC)
             at(2, second_matmul)
             at(0, first_matmul)
             if tick + 2 < NG: transpose_kv(tick + 2)
             at(1, residual_tensor, 0, D)
-            if tick == 4: residual_tensor(3, D, GW, "qc")
+            if tick <= 5: residual_tensor(tick - 1, D, GW, "qc")
             else: at(1, residual_tensor, D, TENSOR_COLS, "qc")
             if 1 <= tick - 4 < NG and tick - 4 not in SHARED: finish(tick - 4)
             at(3, centre)

@@ -23,7 +23,7 @@ BLK = 8
 NB = NT // BLK
 LN_EPS = 1e-5
 FLOPS = 2 * 2 * B * D * D
-TENSOR_COLS = 768
+GP_COLS = 256
 ENGINE_TILES = 16
 
 
@@ -228,9 +228,9 @@ def tile_crossmodalattention_pa_t_kernel(
         def residual_gpsimd(c):
             t, off = q_tiles[GT * c]
             nc.gpsimd.tensor_tensor(
-                out=residual_tile(c)[:, TENSOR_COLS:GW],
-                in0=t[:, off + TENSOR_COLS : off + GW],
-                in1=ob_sb[:, TENSOR_COLS - D : D],
+                out=residual_tile(c)[:, 0:GP_COLS],
+                in0=t[:, off : off + GP_COLS],
+                in1=ob_sb[:, 0:GP_COLS],
                 op=ALU.add,
             )
 
@@ -556,14 +556,14 @@ def tile_crossmodalattention_pa_t_kernel(
         copy_kv(3, vcopy)
         means(0)
         copy_head_weights(12, 16, scopy)
-        residual_tensor(1, 0, D)
-        residual_tensor(1, D, TENSOR_COLS, "qc")
+        residual_tensor(1, GP_COLS, D)
+        residual_tensor(1, D, GW, "qc")
         transpose_kv(4)
         residual_gpsimd(2)
         square(0, 0)
         square(0, 1)
         deviation(0)
-        residual_out(1, 0)
+        residual_out(1, GP_COLS)
         residual_out(1, D)
         centre(0)
         release_gpsimd(2)
@@ -575,9 +575,9 @@ def tile_crossmodalattention_pa_t_kernel(
         finish(0)
         add_residual(1)
         add_value_bias(3)
-        residual_tensor(2, 0, D)
-        residual_tensor(2, D, TENSOR_COLS, "qc")
-        residual_out(2, 0)
+        residual_tensor(2, GP_COLS, D)
+        residual_tensor(2, D, GW, "qc")
+        residual_out(2, GP_COLS)
         residual_out(2, D)
         transpose_kv(5)
 
@@ -607,15 +607,14 @@ def tile_crossmodalattention_pa_t_kernel(
             at(2, second_matmul)
             at(0, first_matmul)
             if tick + 2 < NG: transpose_kv(tick + 2)
-            at(1, residual_tensor, 0, D)
-            if tick <= 5: residual_tensor(tick - 1, D, GW, "qc")
-            else: at(1, residual_tensor, D, TENSOR_COLS, "qc")
+            at(1, residual_tensor, 0 if tick <= 5 else GP_COLS, D)
+            at(1, residual_tensor, D, GW, "qc")
             if 1 <= tick - 4 < NG and tick - 4 not in SHARED: finish(tick - 4)
             at(3, centre)
             if tick == NG: quantise(NG + 1, GC, 2 * GC)
             at(0, add_value_bias)
             if tick != 5: at(3, deviation)
-            if tick != 4: at(1, residual_out, 0)
+            if tick != 4: at(1, residual_out, 0 if tick == 5 else GP_COLS)
             if tick != 4: at(1, residual_out, D)
             if tick - 3 in SHARED: finish_shared(tick - 3)
             at(2, add_residual)

@@ -294,10 +294,10 @@ def tile_crossmodalattention_pa_t_kernel(
                 )
             st["s1", c] = banks
 
-        def add_value_bias(c):
+        def add_value_bias(c, other=None):
             banks = st["s1", c]
             planes = w2.tile([P, 4 * GC], F32, name="planes", tag="planes")
-            for t in reversed(range(4)):
+            for t in (3, 2, 1, 0) if c > 4 else (0, 1, 2, 3):
                 nc.scalar.activation(
                     out=planes[:, t * GC : (t + 1) * GC],
                     in_=banks[t // 2][:, (t % 2) * GC : (t % 2 + 1) * GC],
@@ -305,6 +305,8 @@ def tile_crossmodalattention_pa_t_kernel(
                     bias=bv[:, t : t + 1],
                     scale=1.0,
                 )
+                if t == (3 if c > 4 else 0) and other is not None:
+                    deviation(other)
             st["planes", c] = planes
 
         def weigh_heads_vector(c, lo, hi):
@@ -371,14 +373,14 @@ def tile_crossmodalattention_pa_t_kernel(
                 op=ALU.add,
             )
 
-        def add_residual(c, tiles=(1, 0)):
+        def add_residual(c, tiles=None):
             banks = st["s2", c]
             if ("z", c) not in st:
                 z = w2.tile([P, GW], F32, name="z", tag="z")
                 sums = w3.tile([P, GT], F32, name="sums", tag="sums")
                 st["z", c] = (z, sums)
             z, sums = st["z", c]
-            for jj in tiles:
+            for jj in tiles or ((1, 0) if c > 2 else (0, 1)):
                 nc.vector.scalar_tensor_tensor(
                     out=z[:, jj * D : (jj + 1) * D],
                     in0=banks[jj][:],
@@ -392,38 +394,44 @@ def tile_crossmodalattention_pa_t_kernel(
         def means(c):
             z, sums = st["z", c]
             negmu = w3.tile([P, GT], F32, name="negmu", tag="negmu")
-            nc.scalar.mul(out=negmu[:], in_=sums[:], mul=-1.0 / D)
-            ssq = w3.tile([P, GT], F32, name="ssq", tag="ssq")
-            st["stat", c] = (negmu, ssq)
+            if c < 3 or c >= NG - 3:
+                nc.scalar.mul(out=negmu[:], in_=sums[:], mul=-1.0 / D)
+            else:
+                nc.gpsimd.tensor_scalar(
+                    out=negmu[:], in0=sums[:], scalar1=-1.0 / D, scalar2=0.0, op0=ALU.mult, op1=ALU.add
+                )
+            st["negmu", c] = negmu
 
         def square(c, jj):
             z, sums = st["z", c]
-            negmu, ssq = st["stat", c]
+            if jj == 0:
+                st["ssq", c] = w3.tile([P, GT], F32, name="ssq", tag="ssq")
+            ssq = st["ssq", c]
             junk = w2.tile([P, D], BF16, name="junk", tag="junk")
             nc.scalar.activation(
                 out=junk[:],
                 in_=z[:, jj * D : (jj + 1) * D],
                 func=ACT.Square,
-                bias=negmu[:, jj : jj + 1],
-                scale=1.0,
+                bias=sums[:, jj : jj + 1],
+                scale=-float(D),
                 accum_out=ssq[:, jj : jj + 1],
             )
 
         def deviation(c):
-            negmu, ssq = st["stat", c]
+            ssq = st["ssq", c]
             rstd = w3.tile([P, GT], F32, name="rstd", tag="rstd")
             nc.scalar.activation(
                 out=rstd[:],
                 in_=ssq[:],
                 func=ACT.Abs_reciprocal_sqrt,
                 bias=eps[:, 0:1],
-                scale=1.0 / D,
+                scale=1.0 / D**3,
             )
             st["rstd", c] = rstd
 
         def centre(c):
             z, sums = st["z", c]
-            negmu, ssq = st["stat", c]
+            negmu = st["negmu", c]
             o = w4.tile([P, GW], F32, name="o", tag="o")
             for jj in range(GT):
                 nc.vector.scalar_tensor_tensor(
@@ -595,26 +603,31 @@ def tile_crossmodalattention_pa_t_kernel(
                 load_chunk(q_view, q_tiles, "q", tick // 4 + 4)
             if tick % 4 == 0:
                 load_chunk(kv_view, kv_tiles, "kv", tick // 4 + 4)
-            if tick != 5: at(3, means)
+            if tick == 4 or tick >= NG: at(3, means)
             if tick + 1 < NG: copy_kv(tick + 1, scopy)
             if tick != 5: at(3, square, 0)
             if tick != 5: at(3, square, 1)
             if tick in (4, 5, NG): release_gpsimd(tick - 1)
+            if 5 < tick < NG: at(3, means)
             if tick > 5 and tick < NG: residual_gpsimd(tick)
             if tick - 1 < NG: weigh_heads(tick - 1, nc.gpsimd)
-            if tick == 5: residual_gpsimd(tick)
+            if tick == 5:
+                residual_gpsimd(4)
+                residual_gpsimd(5)
             if tick <= NG: quantise(tick, 0 if tick < NG else GC, 2 * GC)
             at(2, second_matmul)
             at(0, first_matmul)
             if tick + 2 < NG: transpose_kv(tick + 2)
-            at(1, residual_tensor, 0 if tick <= 5 else GP_COLS, D)
+            at(1, residual_tensor, 0 if tick == 4 else GP_COLS, D)
             at(1, residual_tensor, D, GW, "qc")
             if 1 <= tick - 4 < NG and tick - 4 not in SHARED: finish(tick - 4)
             at(3, centre)
             if tick == NG: quantise(NG + 1, GC, 2 * GC)
-            at(0, add_value_bias)
-            if tick != 5: at(3, deviation)
-            if tick != 4: at(1, residual_out, 0 if tick == 5 else GP_COLS)
+            if tick < NG:
+                add_value_bias(tick, tick - 3 if tick != 5 else None)
+            elif tick - 3 < NG:
+                deviation(tick - 3)
+            if tick != 4: at(1, residual_out, GP_COLS)
             if tick != 4: at(1, residual_out, D)
             if tick - 3 in SHARED: finish_shared(tick - 3)
             at(2, add_residual)

@@ -23,7 +23,7 @@ BLK = 8
 NB = NT // BLK
 LN_EPS = 1e-5
 FLOPS = 2 * 2 * B * D * D
-GP_COLS = 256
+GP_COLS = 384
 ENGINE_TILES = 16
 
 
@@ -444,16 +444,15 @@ def tile_crossmodalattention_pa_t_kernel(
                 )
             st["o", c] = o
 
-        def finish_shared(c):
+        def finish_shared(c, jj):
             rstd = st["rstd", c]
             o = st["o", c]
-            for jj in range(GT):
-                lo, hi = jj * D, (jj + 1) * D
-                nc.scalar.activation(
-                    out=o[:, lo:hi], in_=o[:, lo:hi], func=ACT.Copy, scale=rstd[:, jj : jj + 1]
-                )
-                nc.gpsimd.tensor_tensor(out=o[:, lo:hi], in0=o[:, lo:hi], in1=b_sb[:], op=ALU.add)
-                nc.sync.dma_start(out=out_view[:, c * GW + lo : c * GW + hi], in_=o[:, lo:hi])
+            lo, hi = jj * D, (jj + 1) * D
+            nc.scalar.activation(
+                out=o[:, lo:hi], in_=o[:, lo:hi], func=ACT.Copy, scale=rstd[:, jj : jj + 1]
+            )
+            nc.gpsimd.tensor_tensor(out=o[:, lo:hi], in0=o[:, lo:hi], in1=b_sb[:], op=ALU.add)
+            nc.sync.dma_start(out=out_view[:, c * GW + lo : c * GW + hi], in_=o[:, lo:hi])
 
         def finish(c):
             rstd = st["rstd", c]
@@ -468,9 +467,9 @@ def tile_crossmodalattention_pa_t_kernel(
                     op0=ALU.mult,
                     op1=ALU.add,
                 )
-                if c == NG - 1:
+                if c >= NG - 3:
                     nc.sync.dma_start(out=out_view[:, c * GW + lo : c * GW + hi], in_=o[:, lo:hi])
-            if c < NG - 1:
+            if c < NG - 3:
                 nc.sync.dma_start(out=out_view[:, c * GW : (c + 1) * GW], in_=o[:])
 
         vcopy = nc.vector.tensor_copy
@@ -592,45 +591,39 @@ def tile_crossmodalattention_pa_t_kernel(
         residual_tile(3)
         residual_tile(4)
 
-        SHARED = (NG - 3, NG - 2)
-
         def at(lag, fn, *args):
             if 0 <= tick - lag < NG:
                 fn(tick - lag, *args)
 
-        for tick in range(4, NG + 6):
+        for tick in range(4, NG):
             if tick % 4 == 1:
                 load_chunk(q_view, q_tiles, "q", tick // 4 + 4)
             if tick % 4 == 0:
                 load_chunk(kv_view, kv_tiles, "kv", tick // 4 + 4)
-            if tick == 4 or tick >= NG: at(3, means)
+            if tick == 4: means(1)
             if tick + 1 < NG: copy_kv(tick + 1, scopy)
             if tick != 5: at(3, square, 0)
             if tick != 5: at(3, square, 1)
-            if tick in (4, 5, NG): release_gpsimd(tick - 1)
-            if 5 < tick < NG: at(3, means)
-            if tick > 5 and tick < NG: residual_gpsimd(tick)
-            if tick - 1 < NG: weigh_heads(tick - 1, nc.gpsimd)
+            if tick in (4, 5): release_gpsimd(tick - 1)
+            if tick > 5: means(tick - 3)
+            if tick > 5: residual_gpsimd(tick)
+            weigh_heads(tick - 1, nc.gpsimd)
             if tick == 5:
                 residual_gpsimd(4)
                 residual_gpsimd(5)
-            if tick <= NG: quantise(tick, 0 if tick < NG else GC, 2 * GC)
-            at(2, second_matmul)
-            at(0, first_matmul)
+            quantise(tick, 0, 2 * GC)
+            second_matmul(tick - 2)
+            first_matmul(tick)
             if tick + 2 < NG: transpose_kv(tick + 2)
-            at(1, residual_tensor, 0 if tick == 4 else GP_COLS, D)
-            at(1, residual_tensor, D, GW, "qc")
-            if 1 <= tick - 4 < NG and tick - 4 not in SHARED: finish(tick - 4)
-            at(3, centre)
-            if tick == NG: quantise(NG + 1, GC, 2 * GC)
-            if tick < NG:
-                add_value_bias(tick, tick - 3 if tick != 5 else None)
-            elif tick - 3 < NG:
-                deviation(tick - 3)
-            if tick != 4: at(1, residual_out, GP_COLS)
-            if tick != 4: at(1, residual_out, D)
-            if tick - 3 in SHARED: finish_shared(tick - 3)
-            at(2, add_residual)
+            residual_tensor(tick - 1, 0 if tick == 4 else GP_COLS, D)
+            residual_tensor(tick - 1, D, GW, "qc")
+            if tick > 4: finish(tick - 4)
+            centre(tick - 3)
+            add_value_bias(tick, tick - 3 if tick != 5 else None)
+            if 4 < tick < NG - 1:
+                residual_out(tick - 1, GP_COLS)
+                residual_out(tick - 1, D)
+            add_residual(tick - 2)
             if tick == 4:
                 means(2)
                 square(2, 0)
@@ -638,3 +631,38 @@ def tile_crossmodalattention_pa_t_kernel(
                 deviation(2)
                 residual_out(3, 0)
                 residual_out(3, D)
+
+        release_gpsimd(NG - 1)
+        weigh_heads(NG - 1, nc.gpsimd)
+        quantise(NG, GC, 2 * GC)
+        second_matmul(NG - 2)
+        residual_tensor(NG - 1, GP_COLS, D, "s1a")
+        residual_tensor(NG - 1, D, GW, "s1b")
+        means(NG - 3)
+        residual_out(NG - 2, GP_COLS)
+        residual_out(NG - 2, D)
+        square(NG - 3, 0)
+        square(NG - 3, 1)
+        deviation(NG - 3)
+        finish(NG - 4)
+        centre(NG - 3)
+        add_residual(NG - 2)
+        means(NG - 2)
+        quantise(NG + 1, GC, 2 * GC)
+        second_matmul(NG - 1)
+        residual_out(NG - 1, GP_COLS)
+        residual_out(NG - 1, D)
+        square(NG - 2, 0)
+        square(NG - 2, 1)
+        deviation(NG - 2)
+        centre(NG - 2)
+        add_residual(NG - 1)
+        finish(NG - 3)
+        finish_shared(NG - 2, 0)
+        means(NG - 1)
+        finish_shared(NG - 2, 1)
+        square(NG - 1, 0)
+        square(NG - 1, 1)
+        deviation(NG - 1)
+        centre(NG - 1)
+        finish(NG - 1)

@@ -23,7 +23,7 @@ BLK = 8
 NB = NT // BLK
 LN_EPS = 1e-5
 FLOPS = 2 * 2 * B * D * D
-GP_COLS = 384
+GP_COLS = 256
 ENGINE_TILES = 16
 
 
@@ -606,8 +606,8 @@ def tile_crossmodalattention_pa_t_kernel(
             if tick != 5: at(3, square, 1)
             if tick in (4, 5): release_gpsimd(tick - 1)
             if tick > 5: means(tick - 3)
-            if tick > 5: residual_gpsimd(tick)
             weigh_heads(tick - 1, nc.gpsimd)
+            if tick > 5: residual_gpsimd(tick)
             if tick == 5:
                 residual_gpsimd(4)
                 residual_gpsimd(5)

@@ -23,7 +23,7 @@ BLK = 8
 NB = NT // BLK
 LN_EPS = 1e-5
 FLOPS = 2 * 2 * B * D * D
-GP_COLS = 256
+GP_COLS = 320
 ENGINE_TILES = 16
 
 
@@ -205,15 +205,20 @@ def tile_crossmodalattention_pa_t_kernel(
                 start=True,
                 stop=False,
             )
-            for n in range(0, hi - lo, P):
+            n = lo
+            while n < hi:
+                first = n % P
+                end = min(n - first + P, hi)
+                block = n % D - first
                 nc.tensor.matmul(
-                    out=bank[:, n : n + P],
-                    lhsT=ob_cols[:, lo % D + n : lo % D + n + P],
-                    rhs=ident_f[:],
-                    is_transpose=True,
+                    out=bank[:, n - lo : end - lo],
+                    lhsT=ob_cols[:, block : block + P],
+                    rhs=ident_f[:, first : first + end - n],
+                    is_transpose=end - n == P,
                     start=False,
-                    stop=n + P == hi - lo,
+                    stop=end == hi,
                 )
+                n = end
             st["qb", c, lo] = (bank, hi)
 
         def residual_tile(c):

from contextlib import ExitStack

import concourse.mybir as mybir
from concourse.masks import make_identity

F32 = mybir.dt.float32
BF16 = mybir.dt.bfloat16
U32 = mybir.dt.uint32
U8 = mybir.dt.uint8
FP8X4 = mybir.dt.float8_e4m3fn_x4
ALU = mybir.AluOpType
ACT = mybir.ActivationFunctionType

P = 128
B = 8192
D = 512
NT = B // P
GT = 2
NG = NT // GT
GW = GT * D
GC = GT * P
BLK = 8
NB = NT // BLK
LN_EPS = 1e-5
FLOPS = 2 * 2 * B * D * D
GP_COLS = 320
ENGINE_TILES = 16


def tile_crossmodalattention_pa_t_kernel(
    tc, kv_in, q_in, attn_w, w_v, b_v, out_w, out_b, ln_g, ln_b, out
):
    nc = tc.nc
    with ExitStack() as ctx:
        ctx.enter_context(tc.manual_schedule())
        const = ctx.enter_context(tc.tile_pool(name="const", bufs=1))
        w2 = ctx.enter_context(tc.tile_pool(name="w2", bufs=2))
        w3 = ctx.enter_context(tc.tile_pool(name="w3", bufs=3))
        w4 = ctx.enter_context(tc.tile_pool(name="w4", bufs=6))
        psum = ctx.enter_context(tc.psum_pool(name="psum", bufs=1))

        kv_view = kv_in.rearrange("(p j) k -> p (j k)", j=NT)
        q_view = q_in.rearrange("(p j) k -> p (j k)", j=NT)
        out_view = out.rearrange("(p j) n -> p (j n)", j=NT)

        chunks = [(0, 2), (2, 4), (4, 8)] + [(a, a + 8) for a in range(8, NT, 8)]
        kv_tiles = {}
        q_tiles = {}
        st = {}

        def load_chunk(view, store, prefix, k):
            if k >= len(chunks):
                return
            j0, j1 = chunks[k]
            if j1 - j0 < 8:
                t = const.tile([P, (j1 - j0) * D], BF16, name="%s%d" % (prefix, k))
            else:
                t = w3.tile([P, (j1 - j0) * D], BF16, name=prefix + "s", tag=prefix + "s")
            nc.sync.dma_start(out=t[:], in_=view[:, j0 * D : j1 * D])
            for j in range(j0, j1):
                store[j] = (t, (j - j0) * D)

        w_view = w_v.rearrange("(p t) k -> p (t k)", t=4)
        w_halves = []
        for i in range(2):
            half = const.tile([P, 2 * D], BF16, name="w_sb%d" % i)
            nc.sync.dma_start(out=half[:], in_=w_view[:, 2 * i * D : 2 * (i + 1) * D])
            w_halves.append(half)
            if i == 0:
                load_chunk(kv_view, kv_tiles, "kv", 0)
        aw_sb = const.tile([P, NT * 8], BF16, name="aw_sb")
        nc.sync.dma_start(out=aw_sb[:], in_=attn_w.rearrange("(p j) h o -> p (j h o)", j=NT))
        rows = const.tile([P, 3 * D], BF16, name="rows")
        nc.gpsimd.memset(rows[:], 0.0)
        bv_bf = const.tile([P, 4], BF16, name="bv_bf")
        nc.sync.dma_start(out=bv_bf[:], in_=b_v.rearrange("(p t) -> p t", t=4))
        for i, vec in enumerate((ln_g, ln_b, out_b)):
            nc.sync.dma_start(
                out=rows[0:1, i * D : (i + 1) * D], in_=vec.rearrange("(o n) -> o n", o=1)
            )
        load_chunk(q_view, q_tiles, "q", 0)
        ow_sb = const.tile([P, 4 * D], BF16, name="ow_sb")
        nc.sync.dma_start(
            out=ow_sb[:].rearrange("p (nb d) -> p nb d", nb=4),
            in_=out_w.rearrange("(nb p) d -> p nb d", p=P),
        )
        for i in range(1, 5):
            load_chunk(kv_view, kv_tiles, "kv", i)
            load_chunk(q_view, q_tiles, "q", i)

        eps = const.tile([P, 1], F32, name="eps")
        nc.vector.memset(eps[:], LN_EPS)
        warm = const.tile([P, 1], F32, name="warm")
        nc.scalar.activation(out=warm[:], in_=eps[:], func=ACT.Abs_reciprocal_sqrt)
        ones = const.tile([P, P], BF16, name="ones")
        nc.vector.memset(ones[:], 1.0)
        ident_f = const.tile([P, P], F32, name="ident_f")
        make_identity(nc, ident_f[:])
        ident_b = const.tile([P, P], BF16, name="ident_b")
        nc.vector.tensor_copy(out=ident_b[:], in_=ident_f[:])
        awE = const.tile([P, ENGINE_TILES * P], BF16, name="awE")
        awF = const.tile([P, (NT - ENGINE_TILES) * P], F32, name="awF")

        def transpose_weight(words, b, tag, prefix):
            bank = psum.tile([P, D], F32, name=prefix + "T%d" % b, tag=tag)
            for s in range(2):
                for h in range(2):
                    nc.tensor.transpose(
                        bank[:, (s * 2 + h) * P : (s * 2 + h + 1) * P],
                        words(2 * b + s, h),
                        ident_f[:],
                    )
            return bank

        def weight_out(bank, b, grouped, copy):
            copy(
                out=grouped[:].bitcast(F32)[:, b * D : (b + 1) * D].rearrange(
                    "w (s c h) -> w s c h", s=2, h=2
                ),
                in_=bank[:].rearrange("w (s h c) -> w s c h", s=2, h=2),
            )

        def weight_codes(prefix):
            codes = const.tile([P, D], U32, name=prefix + "c", align_bytes=64)
            scales = const.tile([P, D], U8, name=prefix + "s", align_bytes=64)
            return codes, scales

        def quantise_weight(grouped, codes, scales, lo, hi):
            nc.vector.quantize_mx(
                out=codes[:, lo:hi].bitcast(FP8X4), scales=scales[:, lo:hi], in_=grouped[:, 4 * lo : 4 * hi]
            )

        def spread(i, tag, name):
            bank = psum.tile([P, D], F32, name=name, tag=tag)
            nc.tensor.matmul(
                out=bank[:], lhsT=ones[:], rhs=rows[:, i * D : (i + 1) * D], start=True, stop=True
            )
            return bank

        awx = const.tile([P, ENGINE_TILES * P], BF16, name="awx")

        def widen_head_weights(j0, j1, copy):
            copy(
                out=awx[:, j0 * P : j1 * P].rearrange("p (m r) -> p m r", r=16),
                in_=aw_sb[:, j0 * 8 : j1 * 8].unsqueeze(2).to_broadcast([P, (j1 - j0) * 8, 16]),
            )

        def widen_gpsimd(j0, j1):
            nc.gpsimd.tensor_scalar(
                out=awx[:, j0 * P : j1 * P].rearrange("p (m r) -> p m r", r=16),
                in0=aw_sb[:, j0 * 8 : j1 * 8].unsqueeze(2).to_broadcast([P, (j1 - j0) * 8, 16]),
                scalar1=1.0,
                scalar2=0.0,
                op0=ALU.mult,
                op1=ALU.add,
            )

        def transpose_head_weights(j0, j1, tag="kvT"):
            awT = psum.tile([P, BLK * P], BF16, name="awT", tag=tag)
            for j in range(j1 - j0):
                lo = (j0 + j) * P
                nc.tensor.transpose(awT[:, j * P : (j + 1) * P], awx[:, lo : lo + P], ident_b[:])
            st["awT", j0] = awT

        def spread_head_weights():
            nblk = (NT - ENGINE_TILES) // 16
            flat = out.rearrange("r n -> (r n)")
            size = P * 16 * P
            base = B * D - nblk * size
            awT = psum.tile([P, nblk * P], BF16, name="awT2", tag="s2a")
            for i in range(nblk):
                lo = (ENGINE_TILES + 16 * i) * 8
                nc.tensor.transpose(awT[:, i * P : (i + 1) * P], aw_sb[:, lo : lo + P], ident_b[:])
            awS = const.tile([P, nblk * P], F32, name="awS")
            nc.scalar.copy(out=awS[:], in_=awT[:])
            segs = [flat[base + i * size : base + (i + 1) * size] for i in range(nblk)]
            for i in range(nblk):
                nc.sync.dma_start(
                    out=segs[i].rearrange("(q r p) -> q r p", r=16, p=P),
                    in_=awS[:, i * P : (i + 1) * P].unsqueeze(1).to_broadcast([P, 16, P]),
                )
            for i in range(nblk):
                nc.sync.dma_start(
                    out=awF[:, i * 16 * P : (i + 1) * 16 * P].rearrange("q (j p) -> q j p", p=P),
                    in_=segs[i].rearrange("(j q p) -> q j p", j=16, p=P),
                )

        def head_weights(c):
            lo = GT * c * P
            if GT * c < ENGINE_TILES:
                return awE[:, lo : lo + GC]
            lo -= ENGINE_TILES * P
            return awF[:, lo : lo + GC]

        def copy_head_weights(j0, j1, copy):
            copy(out=awE[:, j0 * P : j1 * P], in_=st["awT", j0][:, 0 : (j1 - j0) * P])

        def residual_tensor(c, lo, hi, tag="qb"):
            t, off = q_tiles[GT * c]
            bank = psum.tile([P, D], F32, name="qb", tag=tag)
            nc.tensor.matmul(
                out=bank[:, 0 : hi - lo],
                lhsT=ident_b[:],
                rhs=t[:, off + lo : off + hi],
                start=True,
                stop=False,
            )
            n = lo
            while n < hi:
                first = n % P
                end = min(n - first + P, hi)
                block = n % D - first
                nc.tensor.matmul(
                    out=bank[:, n - lo : end - lo],
                    lhsT=ob_cols[:, block : block + P],
                    rhs=ident_f[:, first : first + end - n],
                    is_transpose=end - n == P,
                    start=False,
                    stop=end == hi,
                )
                n = end
            st["qb", c, lo] = (bank, hi)

        def residual_tile(c):
            if ("qp", c) not in st:
                st["qp", c] = w3.tile([P, GW], F32, name="qp", tag="qp")
            return st["qp", c]

        def residual_out(c, lo):
            bank, hi = st["qb", c, lo]
            nc.scalar.copy(out=residual_tile(c)[:, lo:hi], in_=bank[:, 0 : hi - lo])

        def residual_gpsimd(c):
            t, off = q_tiles[GT * c]
            nc.gpsimd.tensor_tensor(
                out=residual_tile(c)[:, 0:GP_COLS],
                in0=t[:, off : off + GP_COLS],
                in1=ob_sb[:, 0:GP_COLS],
                op=ALU.add,
            )

        def qin(k):
            if ("qin", k) not in st:
                st["qin", k] = w3.tile([P, 8 * GC], BF16, name="qin", tag="qin", align_bytes=64)
            return st["qin", k]

        def attn_half(c):
            return qin(c + 2)[:, 4 * GC : 8 * GC]

        def quantise(k, lo, hi):
            if ("codes", k) not in st:
                codes = w2.tile([P, 2 * GC], U32, name="codes", tag="codes", align_bytes=64)
                scales = w2.tile([P, 2 * GC], U8, name="scales", tag="scales", align_bytes=64)
                st["codes", k] = (codes, scales)
            codes, scales = st["codes", k]
            nc.vector.quantize_mx(
                out=codes[:, lo:hi].bitcast(FP8X4),
                scales=scales[:, lo:hi],
                in_=qin(k)[:, 4 * lo : 4 * hi],
            )

        def transpose_kv(c, tag="kvT"):
            kvT = psum.tile([P, D], F32, name="kvT", tag=tag)
            for jj in range(GT):
                t, off = kv_tiles[GT * c + jj]
                t_f = t[:].bitcast(F32)
                for u in range(2):
                    lo = off // 2
                    nc.tensor.transpose(
                        kvT[:, (jj * 2 + u) * P : (jj * 2 + u + 1) * P],
                        t_f[:, lo + u : lo + 2 * P : 2],
                        ident_f[:],
                    )
            st["kvT", c] = kvT

        def copy_kv(c, copy):
            copy(
                out=qin(c)[:, 0 : 4 * GC]
                .bitcast(F32)
                .rearrange("w (s c h) -> w s c h", s=GT, h=2),
                in_=st["kvT", c][:].rearrange("w (s h c) -> w s c h", s=GT, h=2),
            )

        def first_matmul(c):
            codes, scales = st["codes", c]
            banks = (
                psum.tile([P, D], F32, name="s1a", tag="s1a"),
                psum.tile([P, D], F32, name="s1b", tag="s1b"),
            )
            for t in range(4):
                nc.tensor.matmul_mx(
                    out=banks[t // 2][:, (t % 2) * GC : (t % 2 + 1) * GC],
                    lhsT=wc[:, t * P : (t + 1) * P].bitcast(FP8X4),
                    lhsT_scale=ws[:, t * P : (t + 1) * P],
                    rhs=codes[:, 0:GC].bitcast(FP8X4),
                    rhs_scale=scales[:, 0:GC],
                    start=True,
                    stop=True,
                )
            st["s1", c] = banks

        def add_value_bias(c, other=None):
            banks = st["s1", c]
            planes = w2.tile([P, 4 * GC], F32, name="planes", tag="planes")
            for t in (3, 2, 1, 0) if c > 4 else (0, 1, 2, 3):
                nc.scalar.activation(
                    out=planes[:, t * GC : (t + 1) * GC],
                    in_=banks[t // 2][:, (t % 2) * GC : (t % 2 + 1) * GC],
                    func=ACT.Identity,
                    bias=bv[:, t : t + 1],
                    scale=1.0,
                )
                if t == (3 if c > 4 else 0) and other is not None:
                    deviation(other)
            st["planes", c] = planes

        def weigh_heads_vector(c, lo, hi):
            banks = st["s1", c]
            if lo == 0:
                st["planes_v", c] = w2.tile([P, 4 * GC], BF16, name="planes_v", tag="planes")
            planes = st["planes_v", c]
            for t in range(4):
                nc.vector.scalar_tensor_tensor(
                    out=planes[:, t * GC + lo : t * GC + hi],
                    in0=banks[t // 2][:, (t % 2) * GC + lo : (t % 2) * GC + hi],
                    scalar=bv[:, t : t + 1],
                    in1=head_weights(c)[:, lo:hi],
                    op0=ALU.add,
                    op1=ALU.mult,
                )

        def interleave(c, lo, hi, copy):
            copy(
                out=attn_half(c)[:, 4 * lo : 4 * hi].rearrange("p (c i t) -> p c t i", i=4, t=4),
                in_=st["planes_v", c][:]
                .rearrange("p (t w) -> p t w", t=4)[:, :, lo:hi]
                .rearrange("p t (c i) -> p c t i", i=4),
            )

        def weigh_heads(c, engine):
            engine.tensor_tensor(
                out=attn_half(c).rearrange("p (c i t) -> p c t i", i=4, t=4),
                in0=st["planes", c][:].rearrange("p (t c i) -> p c t i", t=4, i=4),
                in1=head_weights(c)
                .rearrange("p (c i) -> p c i", i=4)
                .unsqueeze(2)
                .to_broadcast([P, GC // 4, 4, 4]),
                op=ALU.mult,
            )

        def release_gpsimd(c):
            nc.vector.tensor_copy(out=attn_half(c)[:, 0:1], in_=attn_half(c - 1)[:, 0:1])

        def second_matmul(c):
            codes, scales = st["codes", c + 2]
            banks = (
                psum.tile([P, D], F32, name="s2a", tag="s2a"),
                psum.tile([P, D], F32, name="s2b", tag="s2b"),
            )
            for jj in range(GT):
                nc.tensor.matmul_mx(
                    out=banks[jj][:],
                    lhsT=codes[:, GC + jj * P : GC + (jj + 1) * P].bitcast(FP8X4),
                    lhsT_scale=scales[:, GC + jj * P : GC + (jj + 1) * P],
                    rhs=oc[:].bitcast(FP8X4),
                    rhs_scale=os_[:],
                    start=True,
                    stop=True,
                )
            st["s2", c] = banks

        def residual_vector(c, jj):
            t, off = q_tiles[GT * c + jj]
            nc.vector.tensor_tensor(
                out=residual_tile(c)[:, jj * D : (jj + 1) * D],
                in0=t[:, off : off + D],
                in1=ob_sb[:],
                op=ALU.add,
            )

        def add_residual(c, tiles=None):
            banks = st["s2", c]
            if ("z", c) not in st:
                z = w2.tile([P, GW], F32, name="z", tag="z")
                sums = w3.tile([P, GT], F32, name="sums", tag="sums")
                st["z", c] = (z, sums)
            z, sums = st["z", c]
            for jj in tiles or ((1, 0) if c > 2 else (0, 1)):
                nc.vector.scalar_tensor_tensor(
                    out=z[:, jj * D : (jj + 1) * D],
                    in0=banks[jj][:],
                    scalar=0.0,
                    in1=st["qp", c][:, jj * D : (jj + 1) * D],
                    op0=ALU.add,
                    op1=ALU.add,
                    accum_out=sums[:, jj : jj + 1],
                )

        def means(c):
            z, sums = st["z", c]
            negmu = w3.tile([P, GT], F32, name="negmu", tag="negmu")
            if c < 3 or c >= NG - 3:
                nc.scalar.mul(out=negmu[:], in_=sums[:], mul=-1.0 / D)
            else:
                nc.gpsimd.tensor_scalar(
                    out=negmu[:], in0=sums[:], scalar1=-1.0 / D, scalar2=0.0, op0=ALU.mult, op1=ALU.add
                )
            st["negmu", c] = negmu

        def square(c, jj):
            z, sums = st["z", c]
            if jj == 0:
                st["ssq", c] = w3.tile([P, GT], F32, name="ssq", tag="ssq")
            ssq = st["ssq", c]
            junk = w2.tile([P, D], BF16, name="junk", tag="junk")
            nc.scalar.activation(
                out=junk[:],
                in_=z[:, jj * D : (jj + 1) * D],
                func=ACT.Square,
                bias=sums[:, jj : jj + 1],
                scale=-float(D),
                accum_out=ssq[:, jj : jj + 1],
            )

        def deviation(c):
            ssq = st["ssq", c]
            rstd = w3.tile([P, GT], F32, name="rstd", tag="rstd")
            nc.scalar.activation(
                out=rstd[:],
                in_=ssq[:],
                func=ACT.Abs_reciprocal_sqrt,
                bias=eps[:, 0:1],
                scale=1.0 / D**3,
            )
            st["rstd", c] = rstd

        def centre(c):
            z, sums = st["z", c]
            negmu = st["negmu", c]
            o = w4.tile([P, GW], F32, name="o", tag="o")
            for jj in range(GT):
                nc.vector.scalar_tensor_tensor(
                    out=o[:, jj * D : (jj + 1) * D],
                    in0=z[:, jj * D : (jj + 1) * D],
                    scalar=negmu[:, jj : jj + 1],
                    in1=gb_ps[:, 0:D],
                    op0=ALU.add,
                    op1=ALU.mult,
                )
            st["o", c] = o

        def finish_shared(c, jj):
            rstd = st["rstd", c]
            o = st["o", c]
            lo, hi = jj * D, (jj + 1) * D
            nc.scalar.activation(
                out=o[:, lo:hi], in_=o[:, lo:hi], func=ACT.Copy, scale=rstd[:, jj : jj + 1]
            )
            nc.gpsimd.tensor_tensor(out=o[:, lo:hi], in0=o[:, lo:hi], in1=b_sb[:], op=ALU.add)
            nc.sync.dma_start(out=out_view[:, c * GW + lo : c * GW + hi], in_=o[:, lo:hi])

        def finish(c):
            rstd = st["rstd", c]
            o = st["o", c]
            for jj in reversed(range(GT)):
                lo, hi = jj * D, (jj + 1) * D
                nc.vector.scalar_tensor_tensor(
                    out=o[:, lo:hi],
                    in0=o[:, lo:hi],
                    scalar=rstd[:, jj : jj + 1],
                    in1=gb_ps[:, D : 2 * D],
                    op0=ALU.mult,
                    op1=ALU.add,
                )
                if c >= NG - 3:
                    nc.sync.dma_start(out=out_view[:, c * GW + lo : c * GW + hi], in_=o[:, lo:hi])
            if c < NG - 3:
                nc.sync.dma_start(out=out_view[:, c * GW : (c + 1) * GW], in_=o[:])

        vcopy = nc.vector.tensor_copy
        scopy = nc.scalar.copy
        ow_f = ow_sb[:].bitcast(F32).rearrange("n (nb q a) -> n nb a q", nb=4, a=2)
        bv = const.tile([P, 4], F32, name="bv")
        wg = const.tile([P, 4 * D], BF16, name="wg", align_bytes=64)
        og = const.tile([P, 4 * D], BF16, name="og", align_bytes=64)
        ob_cols = const.tile([P, D], F32, name="ob_cols")
        ob_sb = const.tile([P, D], BF16, name="ob_sb")
        b_sb = const.tile([P, D], BF16, name="b_sb")

        wc, ws = weight_codes("w")
        oc, os_ = weight_codes("o")

        def w_words(t, u):
            t_f = w_halves[t // 2][:].bitcast(F32)
            return t_f[:, (t % 2) * 256 + u : (t % 2 + 1) * 256 : 2]

        def ow_words(nb, a):
            return ow_f[:, nb, a, :]

        w_a = transpose_weight(w_words, 0, "s1a", "w")
        weight_out(w_a, 0, wg, scopy)
        widen_gpsimd(0, 4)
        transpose_kv(0)
        copy_kv(0, vcopy)
        w_b = transpose_weight(w_words, 1, "s1b", "w")
        quantise_weight(wg, wc, ws, 0, GC)
        weight_out(w_b, 1, wg, scopy)
        transpose_head_weights(0, 4, "qb")
        quantise(0, 0, GC)
        quantise_weight(wg, wc, ws, GC, 2 * GC)
        copy_head_weights(0, 4, scopy)
        nc.scalar.copy(out=bv[:], in_=bv_bf[:])
        ob_ps = spread(2, "gb", "ob_ps")
        first_matmul(0)
        nc.scalar.copy(out=ob_sb[:], in_=ob_ps[:])
        obT = psum.tile([P, D], BF16, name="obT", tag="qc")
        for n in range(4):
            nc.tensor.transpose(
                obT[:, n * P : (n + 1) * P], rows[:, 2 * D + n * P : 2 * D + (n + 1) * P], ident_b[:]
            )
        widen_head_weights(4, 12, scopy)
        nc.scalar.copy(
            out=ob_cols[:].rearrange("p (n m) -> p n m", n=4),
            in_=obT[:].rearrange("p (n m) -> p n m", n=4)[:, :, 0:1].to_broadcast([P, 4, P]),
        )
        spread_head_weights()
        gb_ps = psum.tile([P, 2 * D], BF16, name="gb_ps", tag="gb")
        for i in range(2):
            nc.tensor.matmul(
                out=gb_ps[:, i * D : (i + 1) * D],
                lhsT=ones[:],
                rhs=rows[:, i * D : (i + 1) * D],
                start=True,
                stop=True,
            )
        residual_vector(0, 0)
        transpose_kv(1, "qb")
        copy_kv(1, scopy)
        o_a = transpose_weight(ow_words, 0, "s2a", "o")
        o_b = transpose_weight(ow_words, 1, "s2b", "o")
        transpose_kv(2)
        residual_gpsimd(1)
        weigh_heads_vector(0, 0, P)
        weigh_heads_vector(0, P, GC)
        interleave(0, 0, P, scopy)
        interleave(0, P, GC, scopy)
        weight_out(o_a, 0, og, vcopy)
        quantise(1, 0, GC)
        first_matmul(1)
        weight_out(o_b, 1, og, vcopy)
        copy_kv(2, scopy)
        quantise(2, GC, 2 * GC)
        quantise_weight(og, oc, os_, 0, 2 * GC)
        transpose_head_weights(4, 12, "qb")
        second_matmul(0)
        quantise(2, 0, GC)
        residual_vector(0, 1)
        add_value_bias(1)
        copy_head_weights(4, 12, scopy)
        widen_head_weights(12, 16, scopy)
        nc.scalar.copy(out=b_sb[:], in_=gb_ps[:, D : 2 * D])
        first_matmul(2)
        add_value_bias(2)
        transpose_kv(3, "qc")
        weigh_heads(1, nc.gpsimd)
        transpose_head_weights(12, 16, "kvT")
        add_residual(0)
        copy_kv(3, vcopy)
        means(0)
        copy_head_weights(12, 16, scopy)
        residual_tensor(1, GP_COLS, D)
        residual_tensor(1, D, GW, "qc")
        transpose_kv(4)
        residual_gpsimd(2)
        square(0, 0)
        square(0, 1)
        deviation(0)
        residual_out(1, GP_COLS)
        residual_out(1, D)
        centre(0)
        release_gpsimd(2)
        quantise(3, 0, 2 * GC)
        weigh_heads(2, nc.gpsimd)
        second_matmul(1)
        first_matmul(3)
        copy_kv(4, vcopy)
        finish(0)
        add_residual(1)
        add_value_bias(3)
        residual_tensor(2, GP_COLS, D)
        residual_tensor(2, D, GW, "qc")
        residual_out(2, GP_COLS)
        residual_out(2, D)
        transpose_kv(5)

        residual_tile(3)
        residual_tile(4)

        def at(lag, fn, *args):
            if 0 <= tick - lag < NG:
                fn(tick - lag, *args)

        for tick in range(4, NG):
            if tick % 4 == 1:
                load_chunk(q_view, q_tiles, "q", tick // 4 + 4)
            if tick % 4 == 0:
                load_chunk(kv_view, kv_tiles, "kv", tick // 4 + 4)
            if tick == 4: means(1)
            if tick + 1 < NG: copy_kv(tick + 1, scopy)
            if tick != 5: at(3, square, 0)
            if tick != 5: at(3, square, 1)
            if tick in (4, 5): release_gpsimd(tick - 1)
            if tick > 5: means(tick - 3)
            weigh_heads(tick - 1, nc.gpsimd)
            if tick > 5: residual_gpsimd(tick)
            if tick == 5:
                residual_gpsimd(4)
                residual_gpsimd(5)
            quantise(tick, 0, 2 * GC)
            second_matmul(tick - 2)
            first_matmul(tick)
            if tick + 2 < NG: transpose_kv(tick + 2)
            residual_tensor(tick - 1, 0 if tick == 4 else GP_COLS, D)
            residual_tensor(tick - 1, D, GW, "qc")
            if tick > 4: finish(tick - 4)
            centre(tick - 3)
            add_value_bias(tick, tick - 3 if tick != 5 else None)
            if 4 < tick < NG - 1:
                residual_out(tick - 1, GP_COLS)
                residual_out(tick - 1, D)
            add_residual(tick - 2)
            if tick == 4:
                means(2)
                square(2, 0)
                square(2, 1)
                deviation(2)
                residual_out(3, 0)
                residual_out(3, D)

        release_gpsimd(NG - 1)
        weigh_heads(NG - 1, nc.gpsimd)
        quantise(NG, GC, 2 * GC)
        second_matmul(NG - 2)
        residual_tensor(NG - 1, GP_COLS, D, "s1a")
        residual_tensor(NG - 1, D, GW, "s1b")
        means(NG - 3)
        residual_out(NG - 2, GP_COLS)
        residual_out(NG - 2, D)
        square(NG - 3, 0)
        square(NG - 3, 1)
        deviation(NG - 3)
        finish(NG - 4)
        centre(NG - 3)
        add_residual(NG - 2)
        means(NG - 2)
        quantise(NG + 1, GC, 2 * GC)
        second_matmul(NG - 1)
        residual_out(NG - 1, GP_COLS)
        residual_out(NG - 1, D)
        square(NG - 2, 0)
        square(NG - 2, 1)
        deviation(NG - 2)
        centre(NG - 2)
        add_residual(NG - 1)
        finish(NG - 3)
        finish_shared(NG - 2, 0)
        means(NG - 1)
        finish_shared(NG - 2, 1)
        square(NG - 1, 0)
        square(NG - 1, 1)
        deviation(NG - 1)
        centre(NG - 1)
        finish(NG - 1)
